import numpy as np
import ml_dtypes


def mxq(x, axis, fmt="e4m3"):
    dtype, down = {"e4m3": (ml_dtypes.float8_e4m3fn, 7), "e5m2": (ml_dtypes.float8_e5m2, 14)}[fmt]
    v = np.moveaxis(np.asarray(x, np.float32).astype(ml_dtypes.bfloat16).astype(np.float64), axis, -1)
    blocks = v.reshape(v.shape[:-1] + (-1, 32))
    amax = np.abs(blocks).max(-1, keepdims=True)
    byte = np.maximum(np.where(amax > 0, np.frexp(amax)[1] - 1 + 127, 0) - down, 1)
    scale = np.exp2(byte - 127.0)
    codes = (blocks / scale).astype(np.float32).astype(dtype).astype(np.float64)
    return np.moveaxis((codes * scale).reshape(v.shape), -1, axis)


WIDE = False


def mx_kscale(k):
    if not WIDE:
        return np.ones(k)
    levels = np.array([10, -10, 5, -5, 0])
    a = np.random.permutation(np.resize(levels, k // 512 * 4)).reshape(k // 512, 4)
    idx = np.arange(k)
    return np.exp2(a[idx // 512, idx % 128 // 32])


BF16 = ml_dtypes.bfloat16


def bf(x):
    return np.asarray(x, np.float32).astype(BF16)


def f64(x):
    return np.asarray(x).astype(np.float64)


E2M1 = np.array([0.0, 0.5, 1.0, 1.5, 2.0, 3.0, 4.0, 6.0, -0.0, -0.5, -1.0, -1.5, -2.0, -3.0, -4.0, -6.0])


def pack_weight(w, fmt):
    k, n = w.shape
    w = f64(bf(w)).reshape(k // 32, 32, n)
    amax = np.abs(w).max(1)
    if fmt == "e4m3":
        byte = np.frexp(amax)[1] - 1 + 127 - 7
    else:
        mant, ex = np.frexp(amax / 6.0)
        byte = np.where(mant > 0.5, ex, ex - 1) + 127
    byte = np.clip(np.where(amax > 0, byte, 1), 1, 254)
    scaled = (w * np.exp2(127.0 - byte)[:, None, :]).reshape(k, n).astype(np.float32)
    by_word = np.ascontiguousarray(scaled.reshape(k // 512, 128, 4, n).transpose(0, 1, 3, 2))
    if fmt == "e4m3":
        words = by_word.astype(ml_dtypes.float8_e4m3fn).view(np.uint8)
    else:
        c = by_word.astype(ml_dtypes.float4_e2m1fn).view(np.uint8) & 0xF
        words = c[..., 0::2] | (c[..., 1::2] << 4)
    return np.ascontiguousarray(words), np.ascontiguousarray(byte.astype(np.uint8).reshape(k // 512, 16, n))


def unpack_weight(words, scales, fmt):
    g, p, n, _ = words.shape
    if fmt == "e4m3":
        vals = np.ascontiguousarray(words).view(ml_dtypes.float8_e4m3fn).astype(np.float64)
    else:
        nib = np.empty((g, p, n, 4), np.uint8)
        nib[..., 0::2] = words & 0xF
        nib[..., 1::2] = words >> 4
        vals = E2M1[nib]
    vals = vals * np.repeat(np.exp2(scales.astype(np.float64) - 127.0), 8, axis=1)[..., None]
    return vals.transpose(0, 1, 3, 2).reshape(g * 512, n)

def pack4(w):
    words, scales = pack_weight(w, "e2m1")
    return words.reshape(words.shape[0], 128, -1), scales


def unpack4(words, scales):
    return unpack_weight(words.reshape(words.shape[0], 128, -1, 2), scales, "e2m1")


B, I, H = 256, 16384, 512
G = 2 * H
EPS = 1e-5


def ln(v):
    mu = v.mean(-1, keepdims=True)
    var = np.square(v - mu).mean(-1, keepdims=True)
    return (v - mu) / np.sqrt(var + EPS)


def sigmoid(v):
    return 1.0 / (1.0 + np.exp(-v))


def setup_inputs():
    s, t = mx_kscale(I), mx_kscale(H)
    x = bf(np.random.standard_normal((B, I)) * s)
    h = bf(np.random.standard_normal((B, H)) * t)
    irz_words, irz_scales = pack4((np.random.standard_normal((G, I)) / np.sqrt(I) / s).T)
    b_irz = bf(np.random.standard_normal(G) * 0.5)
    hrz_words, hrz_scales = pack4((np.random.standard_normal((G, H)) / np.sqrt(H) / t).T)
    b_hrz = bf(np.random.standard_normal(G) * 0.5)
    return {"x": x,
            "h": h,
            "W_irz_words": irz_words,
            "W_irz_scales": irz_scales,
            "b_irz": b_irz,
            "W_hrz_words": hrz_words,
            "W_hrz_scales": hrz_scales,
            "b_hrz": b_hrz}


def reference(x, h, W_irz_words, W_irz_scales, b_irz, W_hrz_words, W_hrz_scales, b_hrz):
    i_rz = ln((mxq(f64(x), 1, "e4m3") @ unpack4(W_irz_words, W_irz_scales)) + f64(b_irz))
    h_rz = ln((mxq(f64(h), 1, "e4m3") @ unpack4(W_hrz_words, W_hrz_scales)) + f64(b_hrz))
    return sigmoid(i_rz + h_rz)

@@ -1,0 +1,258 @@
+from contextlib import ExitStack
+
+import concourse.mybir as mybir
+from concourse.masks import make_identity
+
+F32 = mybir.dt.float32
+BF16 = mybir.dt.bfloat16
+I32 = mybir.dt.int32
+U32 = mybir.dt.uint32
+U8 = mybir.dt.uint8
+FP8X4 = mybir.dt.float8_e4m3fn_x4
+FP4X4 = mybir.dt.float4_e2m1fn_x4
+ALU = mybir.AluOpType
+ACT = mybir.ActivationFunctionType
+
+B, I, H, G = 256, 16384, 512, 1024
+EPS = 1e-5
+FLOPS = 2 * B * (I + H) * G
+
+P = 128
+PACK = 4
+K_PASS = P * PACK
+PAIRS = K_PASS // 2
+ROW_TILES = B // P
+N_TILE = 512
+HALVES = G // N_TILE
+SCALE_ROWS = K_PASS // 32
+
+RUN = 4
+CHUNKS = I // (K_PASS * RUN)
+SCALAR_BANKS = 3
+STAGE = 2
+LOADS_AHEAD = 3
+
+
+def load_scale_rows(nc, planes, scales):
+    groups = scales.shape[0]
+    for first in range(0, groups, RUN):
+        some = slice(first, min(first + RUN, groups))
+        for q in range(SCALE_ROWS // 2):
+            partition = 32 * (q // 4) + q % 4
+            nc.sync.dma_start(
+                out=planes[partition:P:64, some, :].bitcast(I32),
+                in_=scales[some, q:SCALE_ROWS:8, :].bitcast(I32).rearrange("g q n -> q g n"),
+            )
+
+
+def transpose_groups(nc, banks, raw, identity):
+    words = raw[:].bitcast(F32)
+    filled = []
+    for g in range(words.shape[2] // PAIRS):
+        bank = banks.tile([P, ROW_TILES, 2, P], F32, name="bank", tag="bank")
+        for r in range(ROW_TILES):
+            for u in range(2):
+                nc.tensor.transpose(
+                    bank[:, r, u, :], words[:, r, g * PAIRS + u : (g + 1) * PAIRS : 2], identity[:]
+                )
+        filled.append(bank)
+    return filled
+
+
+def quantise_groups(nc, filled, grouped, codes, scales):
+    for g, bank in enumerate(filled):
+        side_by_side = grouped[:, g].bitcast(F32)
+        alternately = bank[:].rearrange("p r u b -> p r b u")
+        if g < SCALAR_BANKS:
+            nc.scalar.copy(out=side_by_side, in_=alternately)
+        else:
+            nc.vector.tensor_copy(out=side_by_side, in_=alternately)
+    nc.vector.quantize_mx(
+        out=codes[:].rearrange("p g c -> p (g c)").bitcast(FP8X4),
+        scales=scales[:].rearrange("p g c -> p (g c)"),
+        in_=grouped[:].rearrange("p g r b t -> p (g r b t)"),
+    )
+
+
+def multiply_groups(nc, sums, codes, scales, w_words, w_scales, first, last):
+    groups = codes.shape[1]
+    for r in range(ROW_TILES):
+        rows = slice(r * P, (r + 1) * P)
+        for half in range(HALVES):
+            for g in range(groups):
+                nc.tensor.matmul_mx(
+                    out=sums[r][half][:],
+                    lhsT=codes[:, g, rows].bitcast(FP8X4),
+                    lhsT_scale=scales[:, g, rows],
+                    rhs=w_words[:, g, half * 2 * N_TILE : (half + 1) * 2 * N_TILE].bitcast(FP4X4),
+                    rhs_scale=w_scales[:, g, half * N_TILE : (half + 1) * N_TILE],
+                    start=first and g == 0,
+                    stop=last and g == groups - 1,
+                )
+
+
+def open_sums(psum):
+    return [
+        [
+            psum.tile([P, N_TILE], F32, name="sum%d%d" % (r, half), tag="sum%d%d" % (r, half))
+            for half in range(HALVES)
+        ]
+        for r in range(ROW_TILES)
+    ]
+
+
+def add_bias_and_measure(nc, pool, sums_of_rows, bias, minus_half):
+    v = pool.tile([P, G], F32, name="v")
+    stats = pool.tile([P, HALVES, 6], F32, name="stats")
+    for half in range(HALVES):
+        cols = slice(half * N_TILE, (half + 1) * N_TILE)
+        nc.vector.tensor_tensor(out=v[:, cols], in0=sums_of_rows[half][:], in1=bias[:, cols], op=ALU.add)
+    for half in range(HALVES):
+        cols = slice(half * N_TILE, (half + 1) * N_TILE)
+        nc.vector.bn_stats(out=stats[:, half, :], in_=v[:, cols])
+    mean_var = pool.tile([P, 2], F32, name="mean_var")
+    nc.vector.bn_aggr(out=mean_var[:], in_=stats[:].rearrange("p h s -> p (h s)"))
+    var_eps = pool.tile([P, 1], F32, name="var_eps")
+    nc.vector.tensor_scalar(out=var_eps[:], in0=mean_var[:, 1:2], scalar1=EPS, scalar2=None, op0=ALU.add)
+    rstd = pool.tile([P, 1], F32, name="rstd")
+    nc.gpsimd.tensor_tensor(out=rstd[:], in0=var_eps[:], in1=minus_half[:], op=ALU.pow)
+    shift = pool.tile([P, 1], F32, name="shift")
+    nc.vector.tensor_scalar(
+        out=shift[:], in0=mean_var[:, 0:1], scalar1=rstd[:, 0:1], scalar2=-1.0, op0=ALU.mult, op1=ALU.mult
+    )
+    return v, rstd, shift
+
+
+def tile_layernormgrucell_pa_k_kernel(
+    tc, x, h, W_irz_words, W_irz_scales, b_irz, W_hrz_words, W_hrz_scales, b_hrz, out
+):
+    nc = tc.nc
+    with ExitStack() as ctx:
+        ctx.enter_context(tc.manual_schedule())
+        keep = ctx.enter_context(tc.tile_pool(name="keep", bufs=1))
+        x_pool = ctx.enter_context(tc.tile_pool(name="x", bufs=LOADS_AHEAD + 2))
+        w_pool = ctx.enter_context(tc.tile_pool(name="w", bufs=LOADS_AHEAD + 1))
+        grouped_pool = ctx.enter_context(tc.tile_pool(name="grouped", bufs=2))
+        codes_pool = ctx.enter_context(tc.tile_pool(name="codes", bufs=3))
+        norm_pool = ctx.enter_context(tc.tile_pool(name="norm", bufs=2))
+        out_pool = ctx.enter_context(tc.tile_pool(name="out", bufs=4))
+        sum_banks = ctx.enter_context(tc.psum_pool(name="sums", bufs=1))
+        banks = ctx.enter_context(tc.psum_pool(name="banks", bufs=4))
+
+        bias_rows = keep.tile([P, 2, G], BF16, name="bias_rows")
+        nc.vector.memset(bias_rows[:], 0.0)
+        ones = keep.tile([P, P], BF16, name="ones")
+        nc.vector.memset(ones[:], 1.0)
+        minus_half = keep.tile([P, 1], F32, name="minus_half")
+        nc.vector.memset(minus_half[:], -0.5)
+        zero = keep.tile([P, 1], F32, name="zero")
+        nc.vector.memset(zero[:], 0.0)
+        hrz_scales = keep.tile([P, 1, G], U8, name="hrz_scales", align_bytes=64)
+        nc.vector.memset(hrz_scales[:].bitcast(I32), 0)
+        irz_scales = keep.tile([P, I // K_PASS, G], U8, name="irz_scales", align_bytes=64)
+        nc.vector.memset(irz_scales[:].bitcast(I32), 0)
+        identity = keep.tile([P, P], F32, name="identity")
+        make_identity(nc, identity[:])
+        warm = keep.tile([P, 1], F32, name="warm")
+        nc.scalar.activation(out=warm[:], in_=zero[:], func=ACT.Sigmoid)
+
+        x_rows = x.rearrange("(r p) k -> p r k", p=P)
+        x_raw = {}
+        w_words = {}
+
+        def load_x(c):
+            x_raw[c] = x_pool.tile([P, ROW_TILES, RUN * K_PASS], BF16, name="x_raw")
+            nc.sync.dma_start(out=x_raw[c][:], in_=x_rows[:, :, c * RUN * K_PASS : (c + 1) * RUN * K_PASS])
+
+        def load_w(c):
+            if c % STAGE == 0:
+                some = slice(c * RUN, (c + STAGE) * RUN)
+                load_scale_rows(nc, irz_scales[:, some, :], W_irz_scales[some])
+            w_words[c] = w_pool.tile([P, RUN, 2 * G], U8, name="w_words", align_bytes=64)
+            nc.sync.dma_start(
+                out=w_words[c][:].bitcast(I32),
+                in_=W_irz_words[c * RUN : (c + 1) * RUN].bitcast(I32).rearrange("g p n -> p g n"),
+            )
+            if c + 2 < CHUNKS:
+                load_x(c + 2)
+
+        nc.sync.dma_start(out=bias_rows[0:1, 0, :], in_=b_irz.rearrange("(o n) -> o n", o=1))
+        nc.sync.dma_start(out=bias_rows[0:1, 1, :], in_=b_hrz.rearrange("(o n) -> o n", o=1))
+        h_raw = keep.tile([P, ROW_TILES, H], BF16, name="h_raw")
+        nc.sync.dma_start(out=h_raw[:], in_=h.rearrange("(r p) k -> p r k", p=P))
+        load_scale_rows(nc, hrz_scales, W_hrz_scales)
+        hrz_words = keep.tile([P, 1, 2 * G], U8, name="hrz_words", align_bytes=64)
+        nc.sync.dma_start(
+            out=hrz_words[:].bitcast(I32), in_=W_hrz_words.bitcast(I32).rearrange("g p n -> p g n")
+        )
+        load_x(0)
+        load_x(1)
+        for c in range(LOADS_AHEAD):
+            load_w(c)
+
+        bias = keep.tile([P, 2, G], F32, name="bias")
+        for which in range(2):
+            for half in range(HALVES):
+                cols = slice(half * N_TILE, (half + 1) * N_TILE)
+                spread = banks.tile([P, N_TILE], F32, name="spread", tag="bank")
+                nc.tensor.matmul(out=spread[:], lhsT=ones[:], rhs=bias_rows[:, which, cols], start=True, stop=True)
+                nc.scalar.copy(out=bias[:, which, cols], in_=spread[:])
+
+        h_grouped = keep.tile([P, 1, ROW_TILES, P, PACK], BF16, name="h_grouped", align_bytes=64)
+        h_codes = keep.tile([P, 1, B], U32, name="h_codes", align_bytes=64)
+        h_scales = keep.tile([P, 1, B], U8, name="h_scales", align_bytes=64)
+        quantise_groups(nc, transpose_groups(nc, banks, h_raw, identity), h_grouped, h_codes, h_scales)
+        h_sums = open_sums(sum_banks)
+        multiply_groups(nc, h_sums, h_codes, h_scales, hrz_words, hrz_scales, True, True)
+
+        x_codes = {}
+        x_scales = {}
+
+        def quantise_chunk(c, filled):
+            grouped = grouped_pool.tile([P, RUN, ROW_TILES, P, PACK], BF16, name="grouped", align_bytes=64)
+            x_codes[c] = codes_pool.tile([P, RUN, B], U32, name="x_codes", align_bytes=64)
+            x_scales[c] = codes_pool.tile([P, RUN, B], U8, name="x_scales", align_bytes=64)
+            quantise_groups(nc, filled, grouped, x_codes[c], x_scales[c])
+
+        quantise_chunk(0, transpose_groups(nc, banks, x_raw[0], identity))
+
+        h_norm = keep.tile([P, ROW_TILES, G], F32, name="h_norm")
+        for r in range(ROW_TILES):
+            v, rstd, shift = add_bias_and_measure(nc, norm_pool, h_sums[r], bias[:, 1, :], minus_half)
+            nc.scalar.activation(
+                out=h_norm[:, r, :], in_=v[:], func=ACT.Identity, scale=rstd[:, 0:1], bias=shift[:, 0:1]
+            )
+
+        x_sums = open_sums(sum_banks)
+        for c in range(CHUNKS):
+            if c + 1 < CHUNKS:
+                filled = transpose_groups(nc, banks, x_raw[c + 1], identity)
+            multiply_groups(
+                nc,
+                x_sums,
+                x_codes[c],
+                x_scales[c],
+                w_words[c],
+                irz_scales[:, c * RUN : (c + 1) * RUN, :],
+                c == 0,
+                c == CHUNKS - 1,
+            )
+            if c + 1 < CHUNKS:
+                quantise_chunk(c + 1, filled)
+            if c + LOADS_AHEAD < CHUNKS:
+                load_w(c + LOADS_AHEAD)
+
+        measured = []
+        for r in range(ROW_TILES):
+            measured.append(add_bias_and_measure(nc, norm_pool, x_sums[r], bias[:, 0, :], minus_half))
+        for r in range(ROW_TILES):
+            v, rstd, shift = measured[r]
+            for half in range(HALVES):
+                cols = slice(half * N_TILE, (half + 1) * N_TILE)
+                both = out_pool.tile([P, N_TILE], F32, name="both")
+                nc.vector.scalar_tensor_tensor(
+                    out=both[:], in0=v[:, cols], scalar=rstd[:, 0:1], in1=h_norm[:, r, cols], op0=ALU.mult, op1=ALU.add
+                )
+                gate = out_pool.tile([P, N_TILE], F32, name="gate")
+                nc.scalar.activation(out=gate[:], in_=both[:], func=ACT.Sigmoid, bias=shift[:, 0:1])
+                nc.sync.dma_start(out=out[r * P : (r + 1) * P, cols], in_=gate[:])

@@ -33,16 +33,12 @@ STAGE = 2
 LOADS_AHEAD = 3
 
 
-def load_scale_rows(nc, planes, scales):
-    groups = scales.shape[0]
-    for first in range(0, groups, RUN):
-        some = slice(first, min(first + RUN, groups))
-        for q in range(SCALE_ROWS // 2):
-            partition = 32 * (q // 4) + q % 4
-            nc.sync.dma_start(
-                out=planes[partition:P:64, some, :].bitcast(I32),
-                in_=scales[some, q:SCALE_ROWS:8, :].bitcast(I32).rearrange("g q n -> q g n"),
-            )
+def load_scale_rows(nc, planes, scales, which):
+    for j in which:
+        nc.sync.dma_start(
+            out=planes[j:P:32, :, :].bitcast(I32),
+            in_=scales[:, j:SCALE_ROWS:4, :].bitcast(I32).rearrange("g q n -> q g n"),
+        )
 
 
 def transpose_groups(nc, banks, raw, identity):
@@ -164,29 +160,34 @@ def tile_layernormgrucell_pa_k_kernel(
             x_raw[c] = x_pool.tile([P, ROW_TILES, RUN * K_PASS], BF16, name="x_raw")
             nc.sync.dma_start(out=x_raw[c][:], in_=x_rows[:, :, c * RUN * K_PASS : (c + 1) * RUN * K_PASS])
 
+        def load_stage_scales(stage, which):
+            some = slice(stage * STAGE * RUN, (stage + 1) * STAGE * RUN)
+            load_scale_rows(nc, irz_scales[:, some, :], W_irz_scales[some], which)
+
         def load_w(c):
-            if c % STAGE == 0:
-                some = slice(c * RUN, (c + STAGE) * RUN)
-                load_scale_rows(nc, irz_scales[:, some, :], W_irz_scales[some])
             w_words[c] = w_pool.tile([P, RUN, 2 * G], U8, name="w_words", align_bytes=64)
             nc.sync.dma_start(
                 out=w_words[c][:].bitcast(I32),
                 in_=W_irz_words[c * RUN : (c + 1) * RUN].bitcast(I32).rearrange("g p n -> p g n"),
             )
+            if c // STAGE + 1 < CHUNKS // STAGE:
+                share = 4 // STAGE
+                load_stage_scales(c // STAGE + 1, range(c % STAGE * share, (c % STAGE + 1) * share))
             if c + 2 < CHUNKS:
                 load_x(c + 2)
 
-        nc.sync.dma_start(out=bias_rows[0:1, 0, :], in_=b_irz.rearrange("(o n) -> o n", o=1))
-        nc.sync.dma_start(out=bias_rows[0:1, 1, :], in_=b_hrz.rearrange("(o n) -> o n", o=1))
+        nc.gpsimd.dma_start(out=bias_rows[0:1, 0, :], in_=b_irz.rearrange("(o n) -> o n", o=1))
+        nc.gpsimd.dma_start(out=bias_rows[0:1, 1, :], in_=b_hrz.rearrange("(o n) -> o n", o=1))
         h_raw = keep.tile([P, ROW_TILES, H], BF16, name="h_raw")
         nc.sync.dma_start(out=h_raw[:], in_=h.rearrange("(r p) k -> p r k", p=P))
-        load_scale_rows(nc, hrz_scales, W_hrz_scales)
+        load_scale_rows(nc, hrz_scales, W_hrz_scales, range(4))
         hrz_words = keep.tile([P, 1, 2 * G], U8, name="hrz_words", align_bytes=64)
         nc.sync.dma_start(
             out=hrz_words[:].bitcast(I32), in_=W_hrz_words.bitcast(I32).rearrange("g p n -> p g n")
         )
         load_x(0)
         load_x(1)
+        load_stage_scales(0, range(4))
         for c in range(LOADS_AHEAD):
             load_w(c)
 

@@ -41,16 +41,23 @@ def load_scale_rows(nc, planes, scales, which):
         )
 
 
-def transpose_groups(nc, banks, raw, identity):
-    words = raw[:].bitcast(F32)
+def sort_words(nc, pool, raw):
+    groups = raw.shape[2] // K_PASS
+    sorted_words = pool.tile([P, ROW_TILES, groups, 2, P], F32, name="sorted_words")
+    nc.vector.tensor_copy(
+        out=sorted_words[:].rearrange("b r g u p -> b (r g) u p"),
+        in_=raw[:].bitcast(F32).rearrange("b r (g p u) -> b (r g) u p", p=P, u=2),
+    )
+    return sorted_words
+
+
+def transpose_groups(nc, banks, sorted_words, identity):
     filled = []
-    for g in range(words.shape[2] // PAIRS):
+    for g in range(sorted_words.shape[2]):
         bank = banks.tile([P, ROW_TILES, 2, P], F32, name="bank", tag="bank")
         for r in range(ROW_TILES):
             for u in range(2):
-                nc.tensor.transpose(
-                    bank[:, r, u, :], words[:, r, g * PAIRS + u : (g + 1) * PAIRS : 2], identity[:]
-                )
+                nc.tensor.transpose(bank[:, r, u, :], sorted_words[:, r, g, u, :], identity[:])
         filled.append(bank)
     return filled
 
@@ -128,6 +135,7 @@ def tile_layernormgrucell_pa_k_kernel(
         keep = ctx.enter_context(tc.tile_pool(name="keep", bufs=1))
         x_pool = ctx.enter_context(tc.tile_pool(name="x", bufs=LOADS_AHEAD + 2))
         w_pool = ctx.enter_context(tc.tile_pool(name="w", bufs=LOADS_AHEAD + 1))
+        sorted_pool = ctx.enter_context(tc.tile_pool(name="sorted", bufs=2))
         grouped_pool = ctx.enter_context(tc.tile_pool(name="grouped", bufs=2))
         codes_pool = ctx.enter_context(tc.tile_pool(name="codes", bufs=3))
         norm_pool = ctx.enter_context(tc.tile_pool(name="norm", bufs=2))
@@ -202,7 +210,8 @@ def tile_layernormgrucell_pa_k_kernel(
         h_grouped = keep.tile([P, 1, ROW_TILES, P, PACK], BF16, name="h_grouped", align_bytes=64)
         h_codes = keep.tile([P, 1, B], U32, name="h_codes", align_bytes=64)
         h_scales = keep.tile([P, 1, B], U8, name="h_scales", align_bytes=64)
-        quantise_groups(nc, transpose_groups(nc, banks, h_raw, identity), h_grouped, h_codes, h_scales)
+        h_sorted = sort_words(nc, keep, h_raw)
+        quantise_groups(nc, transpose_groups(nc, banks, h_sorted, identity), h_grouped, h_codes, h_scales)
         h_sums = open_sums(sum_banks)
         multiply_groups(nc, h_sums, h_codes, h_scales, hrz_words, hrz_scales, True, True)
 
@@ -215,7 +224,9 @@ def tile_layernormgrucell_pa_k_kernel(
             x_scales[c] = codes_pool.tile([P, RUN, B], U8, name="x_scales", align_bytes=64)
             quantise_groups(nc, filled, grouped, x_codes[c], x_scales[c])
 
-        quantise_chunk(0, transpose_groups(nc, banks, x_raw[0], identity))
+        x_sorted = {0: sort_words(nc, sorted_pool, x_raw[0])}
+        quantise_chunk(0, transpose_groups(nc, banks, x_sorted[0], identity))
+        x_sorted[1] = sort_words(nc, sorted_pool, x_raw[1])
 
         h_norm = keep.tile([P, ROW_TILES, G], F32, name="h_norm")
         for r in range(ROW_TILES):
@@ -227,7 +238,7 @@ def tile_layernormgrucell_pa_k_kernel(
         x_sums = open_sums(sum_banks)
         for c in range(CHUNKS):
             if c + 1 < CHUNKS:
-                filled = transpose_groups(nc, banks, x_raw[c + 1], identity)
+                filled = transpose_groups(nc, banks, x_sorted[c + 1], identity)
             multiply_groups(
                 nc,
                 x_sums,
@@ -240,6 +251,8 @@ def tile_layernormgrucell_pa_k_kernel(
             )
             if c + 1 < CHUNKS:
                 quantise_chunk(c + 1, filled)
+            if c + 2 < CHUNKS:
+                x_sorted[c + 2] = sort_words(nc, sorted_pool, x_raw[c + 2])
             if c + LOADS_AHEAD < CHUNKS:
                 load_w(c + LOADS_AHEAD)
 

@@ -25,39 +25,35 @@ ROW_TILES = B // P
 N_TILE = 512
 HALVES = G // N_TILE
 SCALE_ROWS = K_PASS // 32
+GROUPS = I // K_PASS
 
-RUN = 4
-CHUNKS = I // (K_PASS * RUN)
+CHUNK = 4
+CHUNKS = GROUPS // CHUNK
+X_BUFFERS = 3
 SCALAR_BANKS = 3
-STAGE = 2
-LOADS_AHEAD = 3
+SCALE_SET = 16
+BLOCK = 8
 
 
-def load_scale_rows(nc, planes, scales, which):
-    for j in which:
+def load_scale_rows(nc, planes, scales):
+    for q in range(SCALE_ROWS // 2):
+        partition = 32 * (q // 4) + q % 4
         nc.sync.dma_start(
-            out=planes[j:P:32, :, :].bitcast(I32),
-            in_=scales[:, j:SCALE_ROWS:4, :].bitcast(I32).rearrange("g q n -> q g n"),
+            out=planes[partition:P:64, :, :].bitcast(I32),
+            in_=scales[:, q:SCALE_ROWS:8, :].bitcast(I32).rearrange("g q n -> q g n"),
         )
 
 
-def sort_words(nc, pool, raw):
-    groups = raw.shape[2] // K_PASS
-    sorted_words = pool.tile([P, ROW_TILES, groups, 2, P], F32, name="sorted_words")
-    nc.vector.tensor_copy(
-        out=sorted_words[:].rearrange("b r g u p -> b (r g) u p"),
-        in_=raw[:].bitcast(F32).rearrange("b r (g p u) -> b (r g) u p", p=P, u=2),
-    )
-    return sorted_words
-
-
-def transpose_groups(nc, banks, sorted_words, identity):
+def transpose_groups(nc, banks, raw, identity):
+    words = raw[:].bitcast(F32)
     filled = []
-    for g in range(sorted_words.shape[2]):
+    for g in range(words.shape[2] // PAIRS):
         bank = banks.tile([P, ROW_TILES, 2, P], F32, name="bank", tag="bank")
         for r in range(ROW_TILES):
             for u in range(2):
-                nc.tensor.transpose(bank[:, r, u, :], sorted_words[:, r, g, u, :], identity[:])
+                nc.tensor.transpose(
+                    bank[:, r, u, :], words[:, r, g * PAIRS + u : (g + 1) * PAIRS : 2], identity[:]
+                )
         filled.append(bank)
     return filled
 
@@ -77,27 +73,26 @@ def quantise_groups(nc, filled, grouped, codes, scales):
     )
 
 
-def multiply_groups(nc, sums, codes, scales, w_words, w_scales, first, last):
-    groups = codes.shape[1]
+def multiply_groups(nc, sums, groups, first, last):
     for r in range(ROW_TILES):
         rows = slice(r * P, (r + 1) * P)
         for half in range(HALVES):
-            for g in range(groups):
+            for i, (codes, scales, w_words, w_scales) in enumerate(groups):
                 nc.tensor.matmul_mx(
                     out=sums[r][half][:],
-                    lhsT=codes[:, g, rows].bitcast(FP8X4),
-                    lhsT_scale=scales[:, g, rows],
-                    rhs=w_words[:, g, half * 2 * N_TILE : (half + 1) * 2 * N_TILE].bitcast(FP4X4),
-                    rhs_scale=w_scales[:, g, half * N_TILE : (half + 1) * N_TILE],
-                    start=first and g == 0,
-                    stop=last and g == groups - 1,
+                    lhsT=codes[:, rows].bitcast(FP8X4),
+                    lhsT_scale=scales[:, rows],
+                    rhs=w_words[:, half * 2 * N_TILE : (half + 1) * 2 * N_TILE].bitcast(FP4X4),
+                    rhs_scale=w_scales[:, half * N_TILE : (half + 1) * N_TILE],
+                    start=first and i == 0,
+                    stop=last and i == len(groups) - 1,
                 )
 
 
-def open_sums(psum):
+def open_sums(psum, name):
     return [
         [
-            psum.tile([P, N_TILE], F32, name="sum%d%d" % (r, half), tag="sum%d%d" % (r, half))
+            psum.tile([P, N_TILE], F32, name="%s%d%d" % (name, r, half), tag="%s%d%d" % (name, r, half))
             for half in range(HALVES)
         ]
         for r in range(ROW_TILES)
@@ -133,15 +128,13 @@ def tile_layernormgrucell_pa_k_kernel(
     with ExitStack() as ctx:
         ctx.enter_context(tc.manual_schedule())
         keep = ctx.enter_context(tc.tile_pool(name="keep", bufs=1))
-        x_pool = ctx.enter_context(tc.tile_pool(name="x", bufs=LOADS_AHEAD + 2))
-        w_pool = ctx.enter_context(tc.tile_pool(name="w", bufs=LOADS_AHEAD + 1))
-        sorted_pool = ctx.enter_context(tc.tile_pool(name="sorted", bufs=2))
+        x_pool = ctx.enter_context(tc.tile_pool(name="x", bufs=X_BUFFERS))
         grouped_pool = ctx.enter_context(tc.tile_pool(name="grouped", bufs=2))
-        codes_pool = ctx.enter_context(tc.tile_pool(name="codes", bufs=3))
+        codes_pool = ctx.enter_context(tc.tile_pool(name="codes", bufs=CHUNKS))
+        w_pool = ctx.enter_context(tc.tile_pool(name="w", bufs=CHUNKS))
+        planes_pool = ctx.enter_context(tc.tile_pool(name="planes", bufs=GROUPS // SCALE_SET))
         norm_pool = ctx.enter_context(tc.tile_pool(name="norm", bufs=2))
-        out_pool = ctx.enter_context(tc.tile_pool(name="out", bufs=4))
-        sum_banks = ctx.enter_context(tc.psum_pool(name="sums", bufs=1))
-        banks = ctx.enter_context(tc.psum_pool(name="banks", bufs=4))
+        out_pool = ctx.enter_context(tc.tile_pool(name="out", bufs=2))
 
         bias_rows = keep.tile([P, 2, G], BF16, name="bias_rows")
         nc.vector.memset(bias_rows[:], 0.0)
@@ -151,122 +144,113 @@ def tile_layernormgrucell_pa_k_kernel(
         nc.vector.memset(minus_half[:], -0.5)
         zero = keep.tile([P, 1], F32, name="zero")
         nc.vector.memset(zero[:], 0.0)
-        hrz_scales = keep.tile([P, 1, G], U8, name="hrz_scales", align_bytes=64)
-        nc.vector.memset(hrz_scales[:].bitcast(I32), 0)
-        irz_scales = keep.tile([P, I // K_PASS, G], U8, name="irz_scales", align_bytes=64)
-        nc.vector.memset(irz_scales[:].bitcast(I32), 0)
         identity = keep.tile([P, P], F32, name="identity")
         make_identity(nc, identity[:])
         warm = keep.tile([P, 1], F32, name="warm")
         nc.scalar.activation(out=warm[:], in_=zero[:], func=ACT.Sigmoid)
+        hrz_scales = keep.tile([P, 1, G], U8, name="hrz_scales", align_bytes=64)
+        nc.vector.memset(hrz_scales[:].bitcast(I32), 0)
+        irz_scales = []
+        for s in range(GROUPS // SCALE_SET):
+            irz_scales.append(planes_pool.tile([P, SCALE_SET, G], U8, name="irz_scales", align_bytes=64))
+            nc.vector.memset(irz_scales[s][:].bitcast(I32), 0)
 
         x_rows = x.rearrange("(r p) k -> p r k", p=P)
         x_raw = {}
-        w_words = {}
 
         def load_x(c):
-            x_raw[c] = x_pool.tile([P, ROW_TILES, RUN * K_PASS], BF16, name="x_raw")
-            nc.sync.dma_start(out=x_raw[c][:], in_=x_rows[:, :, c * RUN * K_PASS : (c + 1) * RUN * K_PASS])
+            x_raw[c] = x_pool.tile([P, ROW_TILES, CHUNK * K_PASS], BF16, name="x_raw")
+            nc.sync.dma_start(out=x_raw[c][:], in_=x_rows[:, :, c * CHUNK * K_PASS : (c + 1) * CHUNK * K_PASS])
 
-        def load_stage_scales(stage, which):
-            some = slice(stage * STAGE * RUN, (stage + 1) * STAGE * RUN)
-            load_scale_rows(nc, irz_scales[:, some, :], W_irz_scales[some], which)
-
-        def load_w(c):
-            w_words[c] = w_pool.tile([P, RUN, 2 * G], U8, name="w_words", align_bytes=64)
-            nc.sync.dma_start(
-                out=w_words[c][:].bitcast(I32),
-                in_=W_irz_words[c * RUN : (c + 1) * RUN].bitcast(I32).rearrange("g p n -> p g n"),
-            )
-            if c // STAGE + 1 < CHUNKS // STAGE:
-                share = 4 // STAGE
-                load_stage_scales(c // STAGE + 1, range(c % STAGE * share, (c % STAGE + 1) * share))
-            if c + 2 < CHUNKS:
-                load_x(c + 2)
-
-        nc.gpsimd.dma_start(out=bias_rows[0:1, 0, :], in_=b_irz.rearrange("(o n) -> o n", o=1))
-        nc.gpsimd.dma_start(out=bias_rows[0:1, 1, :], in_=b_hrz.rearrange("(o n) -> o n", o=1))
+        nc.sync.dma_start(out=bias_rows[0:1, 0, :], in_=b_irz.rearrange("(o n) -> o n", o=1))
+        nc.sync.dma_start(out=bias_rows[0:1, 1, :], in_=b_hrz.rearrange("(o n) -> o n", o=1))
         h_raw = keep.tile([P, ROW_TILES, H], BF16, name="h_raw")
         nc.sync.dma_start(out=h_raw[:], in_=h.rearrange("(r p) k -> p r k", p=P))
-        load_scale_rows(nc, hrz_scales, W_hrz_scales, range(4))
+        for c in range(X_BUFFERS):
+            load_x(c)
+
+        bias = keep.tile([P, 2, G], F32, name="bias")
+        h_grouped = keep.tile([P, 1, ROW_TILES, P, PACK], BF16, name="h_grouped", align_bytes=64)
+        h_codes = keep.tile([P, 1, B], U32, name="h_codes", align_bytes=64)
+        h_scales = keep.tile([P, 1, B], U8, name="h_scales", align_bytes=64)
+        x_codes = []
+        x_scales = []
+        with tc.psum_pool(name="banks", bufs=8) as banks:
+            for which in range(2):
+                for half in range(HALVES):
+                    cols = slice(half * N_TILE, (half + 1) * N_TILE)
+                    spread = banks.tile([P, N_TILE], F32, name="spread", tag="bank")
+                    nc.tensor.matmul(
+                        out=spread[:], lhsT=ones[:], rhs=bias_rows[:, which, cols], start=True, stop=True
+                    )
+                    nc.scalar.copy(out=bias[:, which, cols], in_=spread[:])
+
+            quantise_groups(nc, transpose_groups(nc, banks, h_raw, identity), h_grouped, h_codes, h_scales)
+
+            for c in range(CHUNKS):
+                filled = transpose_groups(nc, banks, x_raw[c], identity)
+                grouped = grouped_pool.tile([P, CHUNK, ROW_TILES, P, PACK], BF16, name="grouped", align_bytes=64)
+                x_codes.append(codes_pool.tile([P, CHUNK, B], U32, name="x_codes", align_bytes=64))
+                x_scales.append(codes_pool.tile([P, CHUNK, B], U8, name="x_scales", align_bytes=64))
+                quantise_groups(nc, filled, grouped, x_codes[c], x_scales[c])
+                if c + X_BUFFERS < CHUNKS:
+                    load_x(c + X_BUFFERS)
+
+        load_scale_rows(nc, hrz_scales, W_hrz_scales)
         hrz_words = keep.tile([P, 1, 2 * G], U8, name="hrz_words", align_bytes=64)
         nc.sync.dma_start(
             out=hrz_words[:].bitcast(I32), in_=W_hrz_words.bitcast(I32).rearrange("g p n -> p g n")
         )
-        load_x(0)
-        load_x(1)
-        load_stage_scales(0, range(4))
-        for c in range(LOADS_AHEAD):
-            load_w(c)
-
-        bias = keep.tile([P, 2, G], F32, name="bias")
-        for which in range(2):
-            for half in range(HALVES):
-                cols = slice(half * N_TILE, (half + 1) * N_TILE)
-                spread = banks.tile([P, N_TILE], F32, name="spread", tag="bank")
-                nc.tensor.matmul(out=spread[:], lhsT=ones[:], rhs=bias_rows[:, which, cols], start=True, stop=True)
-                nc.scalar.copy(out=bias[:, which, cols], in_=spread[:])
-
-        h_grouped = keep.tile([P, 1, ROW_TILES, P, PACK], BF16, name="h_grouped", align_bytes=64)
-        h_codes = keep.tile([P, 1, B], U32, name="h_codes", align_bytes=64)
-        h_scales = keep.tile([P, 1, B], U8, name="h_scales", align_bytes=64)
-        h_sorted = sort_words(nc, keep, h_raw)
-        quantise_groups(nc, transpose_groups(nc, banks, h_sorted, identity), h_grouped, h_codes, h_scales)
-        h_sums = open_sums(sum_banks)
-        multiply_groups(nc, h_sums, h_codes, h_scales, hrz_words, hrz_scales, True, True)
-
-        x_codes = {}
-        x_scales = {}
-
-        def quantise_chunk(c, filled):
-            grouped = grouped_pool.tile([P, RUN, ROW_TILES, P, PACK], BF16, name="grouped", align_bytes=64)
-            x_codes[c] = codes_pool.tile([P, RUN, B], U32, name="x_codes", align_bytes=64)
-            x_scales[c] = codes_pool.tile([P, RUN, B], U8, name="x_scales", align_bytes=64)
-            quantise_groups(nc, filled, grouped, x_codes[c], x_scales[c])
-
-        x_sorted = {0: sort_words(nc, sorted_pool, x_raw[0])}
-        quantise_chunk(0, transpose_groups(nc, banks, x_sorted[0], identity))
-        x_sorted[1] = sort_words(nc, sorted_pool, x_raw[1])
-
-        h_norm = keep.tile([P, ROW_TILES, G], F32, name="h_norm")
-        for r in range(ROW_TILES):
-            v, rstd, shift = add_bias_and_measure(nc, norm_pool, h_sums[r], bias[:, 1, :], minus_half)
-            nc.scalar.activation(
-                out=h_norm[:, r, :], in_=v[:], func=ACT.Identity, scale=rstd[:, 0:1], bias=shift[:, 0:1]
-            )
-
-        x_sums = open_sums(sum_banks)
+        w_words = []
         for c in range(CHUNKS):
-            if c + 1 < CHUNKS:
-                filled = transpose_groups(nc, banks, x_sorted[c + 1], identity)
-            multiply_groups(
-                nc,
-                x_sums,
-                x_codes[c],
-                x_scales[c],
-                w_words[c],
-                irz_scales[:, c * RUN : (c + 1) * RUN, :],
-                c == 0,
-                c == CHUNKS - 1,
+            if c * CHUNK % SCALE_SET == 0:
+                s = c * CHUNK // SCALE_SET
+                load_scale_rows(nc, irz_scales[s], W_irz_scales[s * SCALE_SET : (s + 1) * SCALE_SET])
+            w_words.append(w_pool.tile([P, CHUNK, 2 * G], U8, name="w_words", align_bytes=64))
+            nc.sync.dma_start(
+                out=w_words[c][:].bitcast(I32),
+                in_=W_irz_words[c * CHUNK : (c + 1) * CHUNK].bitcast(I32).rearrange("g p n -> p g n"),
             )
-            if c + 1 < CHUNKS:
-                quantise_chunk(c + 1, filled)
-            if c + 2 < CHUNKS:
-                x_sorted[c + 2] = sort_words(nc, sorted_pool, x_raw[c + 2])
-            if c + LOADS_AHEAD < CHUNKS:
-                load_w(c + LOADS_AHEAD)
 
-        measured = []
-        for r in range(ROW_TILES):
-            measured.append(add_bias_and_measure(nc, norm_pool, x_sums[r], bias[:, 0, :], minus_half))
-        for r in range(ROW_TILES):
-            v, rstd, shift = measured[r]
-            for half in range(HALVES):
-                cols = slice(half * N_TILE, (half + 1) * N_TILE)
-                both = out_pool.tile([P, N_TILE], F32, name="both")
-                nc.vector.scalar_tensor_tensor(
-                    out=both[:], in0=v[:, cols], scalar=rstd[:, 0:1], in1=h_norm[:, r, cols], op0=ALU.mult, op1=ALU.add
+        x_groups = [
+            (
+                x_codes[g // CHUNK][:, g % CHUNK, :],
+                x_scales[g // CHUNK][:, g % CHUNK, :],
+                w_words[g // CHUNK][:, g % CHUNK, :],
+                irz_scales[g // SCALE_SET][:, g % SCALE_SET, :],
+            )
+            for g in range(GROUPS)
+        ]
+        h_groups = [(h_codes[:, 0, :], h_scales[:, 0, :], hrz_words[:, 0, :], hrz_scales[:, 0, :])]
+
+        with tc.psum_pool(name="sums", bufs=1) as sum_banks:
+            h_sums = open_sums(sum_banks, "h")
+            multiply_groups(nc, h_sums, h_groups, True, True)
+
+            h_norm = keep.tile([P, ROW_TILES, G], F32, name="h_norm")
+            for r in range(ROW_TILES):
+                v, rstd, shift = add_bias_and_measure(nc, norm_pool, h_sums[r], bias[:, 1, :], minus_half)
+                nc.scalar.activation(
+                    out=h_norm[:, r, :], in_=v[:], func=ACT.Identity, scale=rstd[:, 0:1], bias=shift[:, 0:1]
                 )
-                gate = out_pool.tile([P, N_TILE], F32, name="gate")
-                nc.scalar.activation(out=gate[:], in_=both[:], func=ACT.Sigmoid, bias=shift[:, 0:1])
-                nc.sync.dma_start(out=out[r * P : (r + 1) * P, cols], in_=gate[:])
+
+            x_sums = open_sums(sum_banks, "x")
+            for g in range(0, GROUPS, BLOCK):
+                multiply_groups(nc, x_sums, x_groups[g : g + BLOCK], g == 0, g + BLOCK == GROUPS)
+
+            for r in range(ROW_TILES):
+                v, rstd, shift = add_bias_and_measure(nc, norm_pool, x_sums[r], bias[:, 0, :], minus_half)
+                for half in range(HALVES):
+                    cols = slice(half * N_TILE, (half + 1) * N_TILE)
+                    both = out_pool.tile([P, N_TILE], F32, name="both")
+                    nc.vector.scalar_tensor_tensor(
+                        out=both[:],
+                        in0=v[:, cols],
+                        scalar=rstd[:, 0:1],
+                        in1=h_norm[:, r, cols],
+                        op0=ALU.mult,
+                        op1=ALU.add,
+                    )
+                    gate = out_pool.tile([P, N_TILE], F32, name="gate")
+                    nc.scalar.activation(out=gate[:], in_=both[:], func=ACT.Sigmoid, bias=shift[:, 0:1])
+                    nc.sync.dma_start(out=out[r * P : (r + 1) * P, cols], in_=gate[:])

@@ -29,10 +29,12 @@ GROUPS = I // K_PASS
 
 CHUNK = 4
 CHUNKS = GROUPS // CHUNK
-X_BUFFERS = 3
+ROUNDS = 2
+ROUND_CHUNKS = CHUNKS // ROUNDS
 SCALAR_BANKS = 3
-SCALE_SET = 16
 BLOCK = 8
+BLOCKS = GROUPS // BLOCK
+BLOCK_CHUNKS = BLOCK // CHUNK
 
 
 def load_scale_rows(nc, planes, scales):
@@ -105,8 +107,6 @@ def add_bias_and_measure(nc, pool, sums_of_rows, bias, minus_half):
     for half in range(HALVES):
         cols = slice(half * N_TILE, (half + 1) * N_TILE)
         nc.vector.tensor_tensor(out=v[:, cols], in0=sums_of_rows[half][:], in1=bias[:, cols], op=ALU.add)
-    for half in range(HALVES):
-        cols = slice(half * N_TILE, (half + 1) * N_TILE)
         nc.vector.bn_stats(out=stats[:, half, :], in_=v[:, cols])
     mean_var = pool.tile([P, 2], F32, name="mean_var")
     nc.vector.bn_aggr(out=mean_var[:], in_=stats[:].rearrange("p h s -> p (h s)"))
@@ -128,13 +128,15 @@ def tile_layernormgrucell_pa_k_kernel(
     with ExitStack() as ctx:
         ctx.enter_context(tc.manual_schedule())
         keep = ctx.enter_context(tc.tile_pool(name="keep", bufs=1))
-        x_pool = ctx.enter_context(tc.tile_pool(name="x", bufs=X_BUFFERS))
+        x_pool = ctx.enter_context(tc.tile_pool(name="x", bufs=ROUND_CHUNKS))
         grouped_pool = ctx.enter_context(tc.tile_pool(name="grouped", bufs=2))
         codes_pool = ctx.enter_context(tc.tile_pool(name="codes", bufs=CHUNKS))
         w_pool = ctx.enter_context(tc.tile_pool(name="w", bufs=CHUNKS))
-        planes_pool = ctx.enter_context(tc.tile_pool(name="planes", bufs=GROUPS // SCALE_SET))
+        planes_pool = ctx.enter_context(tc.tile_pool(name="planes", bufs=BLOCKS))
         norm_pool = ctx.enter_context(tc.tile_pool(name="norm", bufs=2))
         out_pool = ctx.enter_context(tc.tile_pool(name="out", bufs=2))
+        sum_banks = ctx.enter_context(tc.psum_pool(name="sums", bufs=1))
+        banks = ctx.enter_context(tc.psum_pool(name="banks", bufs=4))
 
         bias_rows = keep.tile([P, 2, G], BF16, name="bias_rows")
         nc.vector.memset(bias_rows[:], 0.0)
@@ -148,109 +150,114 @@ def tile_layernormgrucell_pa_k_kernel(
         make_identity(nc, identity[:])
         warm = keep.tile([P, 1], F32, name="warm")
         nc.scalar.activation(out=warm[:], in_=zero[:], func=ACT.Sigmoid)
+        irz_scales = []
+        for j in range(BLOCKS):
+            irz_scales.append(planes_pool.tile([P, BLOCK, G], U8, name="irz_scales", align_bytes=64))
+            nc.vector.memset(irz_scales[j][:].bitcast(I32), 0)
         hrz_scales = keep.tile([P, 1, G], U8, name="hrz_scales", align_bytes=64)
         nc.vector.memset(hrz_scales[:].bitcast(I32), 0)
-        irz_scales = []
-        for s in range(GROUPS // SCALE_SET):
-            irz_scales.append(planes_pool.tile([P, SCALE_SET, G], U8, name="irz_scales", align_bytes=64))
-            nc.vector.memset(irz_scales[s][:].bitcast(I32), 0)
 
         x_rows = x.rearrange("(r p) k -> p r k", p=P)
         x_raw = {}
+        x_groups = []
+        w_groups = []
 
-        def load_x(c):
-            x_raw[c] = x_pool.tile([P, ROW_TILES, CHUNK * K_PASS], BF16, name="x_raw")
-            nc.sync.dma_start(out=x_raw[c][:], in_=x_rows[:, :, c * CHUNK * K_PASS : (c + 1) * CHUNK * K_PASS])
+        def load_x(j):
+            for c in range(j * ROUND_CHUNKS, (j + 1) * ROUND_CHUNKS):
+                x_raw[c] = x_pool.tile([P, ROW_TILES, CHUNK * K_PASS], BF16, name="x_raw")
+                nc.sync.dma_start(
+                    out=x_raw[c][:], in_=x_rows[:, :, c * CHUNK * K_PASS : (c + 1) * CHUNK * K_PASS]
+                )
+
+        def load_w(j):
+            load_scale_rows(nc, irz_scales[j], W_irz_scales[j * BLOCK : (j + 1) * BLOCK])
+            for c in range(j * BLOCK_CHUNKS, (j + 1) * BLOCK_CHUNKS):
+                w_words = w_pool.tile([P, CHUNK, 2 * G], U8, name="w_words", align_bytes=64)
+                nc.sync.dma_start(
+                    out=w_words[:].bitcast(I32),
+                    in_=W_irz_words[c * CHUNK : (c + 1) * CHUNK].bitcast(I32).rearrange("g p n -> p g n"),
+                )
+                for g in range(CHUNK):
+                    w_groups.append((w_words[:, g, :], irz_scales[j][:, (c * CHUNK + g) % BLOCK, :]))
+
+        def prepare_x(j):
+            for c in range(j * ROUND_CHUNKS, (j + 1) * ROUND_CHUNKS):
+                filled = transpose_groups(nc, banks, x_raw[c], identity)
+                grouped = grouped_pool.tile([P, CHUNK, ROW_TILES, P, PACK], BF16, name="grouped", align_bytes=64)
+                x_codes = codes_pool.tile([P, CHUNK, B], U32, name="x_codes", align_bytes=64)
+                x_scales = codes_pool.tile([P, CHUNK, B], U8, name="x_scales", align_bytes=64)
+                quantise_groups(nc, filled, grouped, x_codes, x_scales)
+                for g in range(CHUNK):
+                    x_groups.append((x_codes[:, g, :], x_scales[:, g, :]))
+
+        x_sums = open_sums(sum_banks, "x")
+
+        def multiply_x(j):
+            some = range(j * BLOCK, (j + 1) * BLOCK)
+            multiply_groups(nc, x_sums, [x_groups[g] + w_groups[g] for g in some], j == 0, j == BLOCKS - 1)
 
         nc.sync.dma_start(out=bias_rows[0:1, 0, :], in_=b_irz.rearrange("(o n) -> o n", o=1))
         nc.sync.dma_start(out=bias_rows[0:1, 1, :], in_=b_hrz.rearrange("(o n) -> o n", o=1))
         h_raw = keep.tile([P, ROW_TILES, H], BF16, name="h_raw")
         nc.sync.dma_start(out=h_raw[:], in_=h.rearrange("(r p) k -> p r k", p=P))
-        for c in range(X_BUFFERS):
-            load_x(c)
-
-        bias = keep.tile([P, 2, G], F32, name="bias")
-        h_grouped = keep.tile([P, 1, ROW_TILES, P, PACK], BF16, name="h_grouped", align_bytes=64)
-        h_codes = keep.tile([P, 1, B], U32, name="h_codes", align_bytes=64)
-        h_scales = keep.tile([P, 1, B], U8, name="h_scales", align_bytes=64)
-        x_codes = []
-        x_scales = []
-        with tc.psum_pool(name="banks", bufs=8) as banks:
-            for which in range(2):
-                for half in range(HALVES):
-                    cols = slice(half * N_TILE, (half + 1) * N_TILE)
-                    spread = banks.tile([P, N_TILE], F32, name="spread", tag="bank")
-                    nc.tensor.matmul(
-                        out=spread[:], lhsT=ones[:], rhs=bias_rows[:, which, cols], start=True, stop=True
-                    )
-                    nc.scalar.copy(out=bias[:, which, cols], in_=spread[:])
-
-            quantise_groups(nc, transpose_groups(nc, banks, h_raw, identity), h_grouped, h_codes, h_scales)
-
-            for c in range(CHUNKS):
-                filled = transpose_groups(nc, banks, x_raw[c], identity)
-                grouped = grouped_pool.tile([P, CHUNK, ROW_TILES, P, PACK], BF16, name="grouped", align_bytes=64)
-                x_codes.append(codes_pool.tile([P, CHUNK, B], U32, name="x_codes", align_bytes=64))
-                x_scales.append(codes_pool.tile([P, CHUNK, B], U8, name="x_scales", align_bytes=64))
-                quantise_groups(nc, filled, grouped, x_codes[c], x_scales[c])
-                if c + X_BUFFERS < CHUNKS:
-                    load_x(c + X_BUFFERS)
-
+        load_x(0)
+        load_w(0)
         load_scale_rows(nc, hrz_scales, W_hrz_scales)
         hrz_words = keep.tile([P, 1, 2 * G], U8, name="hrz_words", align_bytes=64)
         nc.sync.dma_start(
             out=hrz_words[:].bitcast(I32), in_=W_hrz_words.bitcast(I32).rearrange("g p n -> p g n")
         )
-        w_words = []
-        for c in range(CHUNKS):
-            if c * CHUNK % SCALE_SET == 0:
-                s = c * CHUNK // SCALE_SET
-                load_scale_rows(nc, irz_scales[s], W_irz_scales[s * SCALE_SET : (s + 1) * SCALE_SET])
-            w_words.append(w_pool.tile([P, CHUNK, 2 * G], U8, name="w_words", align_bytes=64))
-            nc.sync.dma_start(
-                out=w_words[c][:].bitcast(I32),
-                in_=W_irz_words[c * CHUNK : (c + 1) * CHUNK].bitcast(I32).rearrange("g p n -> p g n"),
-            )
+        load_w(1)
 
-        x_groups = [
-            (
-                x_codes[g // CHUNK][:, g % CHUNK, :],
-                x_scales[g // CHUNK][:, g % CHUNK, :],
-                w_words[g // CHUNK][:, g % CHUNK, :],
-                irz_scales[g // SCALE_SET][:, g % SCALE_SET, :],
-            )
-            for g in range(GROUPS)
+        bias = keep.tile([P, 2, G], F32, name="bias")
+        for which in range(2):
+            for half in range(HALVES):
+                cols = slice(half * N_TILE, (half + 1) * N_TILE)
+                spread = banks.tile([P, N_TILE], F32, name="spread", tag="bank")
+                nc.tensor.matmul(out=spread[:], lhsT=ones[:], rhs=bias_rows[:, which, cols], start=True, stop=True)
+                nc.scalar.copy(out=bias[:, which, cols], in_=spread[:])
+
+        h_grouped = keep.tile([P, 1, ROW_TILES, P, PACK], BF16, name="h_grouped", align_bytes=64)
+        h_codes = keep.tile([P, 1, B], U32, name="h_codes", align_bytes=64)
+        h_scales = keep.tile([P, 1, B], U8, name="h_scales", align_bytes=64)
+        quantise_groups(nc, transpose_groups(nc, banks, h_raw, identity), h_grouped, h_codes, h_scales)
+        prepare_x(0)
+        load_x(1)
+        load_w(2)
+        load_w(3)
+        multiply_x(0)
+
+        h_sums = [
+            [banks.tile([P, N_TILE], F32, name="h_sum", tag="bank") for half in range(HALVES)]
+            for r in range(ROW_TILES)
         ]
         h_groups = [(h_codes[:, 0, :], h_scales[:, 0, :], hrz_words[:, 0, :], hrz_scales[:, 0, :])]
+        multiply_groups(nc, h_sums, h_groups, True, True)
+        h_norm = keep.tile([P, ROW_TILES, G], F32, name="h_norm")
+        for r in range(ROW_TILES):
+            v, rstd, shift = add_bias_and_measure(nc, norm_pool, h_sums[r], bias[:, 1, :], minus_half)
+            nc.scalar.activation(
+                out=h_norm[:, r, :], in_=v[:], func=ACT.Identity, scale=rstd[:, 0:1], bias=shift[:, 0:1]
+            )
+        multiply_x(1)
 
-        with tc.psum_pool(name="sums", bufs=1) as sum_banks:
-            h_sums = open_sums(sum_banks, "h")
-            multiply_groups(nc, h_sums, h_groups, True, True)
+        prepare_x(1)
+        multiply_x(2)
+        multiply_x(3)
 
-            h_norm = keep.tile([P, ROW_TILES, G], F32, name="h_norm")
-            for r in range(ROW_TILES):
-                v, rstd, shift = add_bias_and_measure(nc, norm_pool, h_sums[r], bias[:, 1, :], minus_half)
-                nc.scalar.activation(
-                    out=h_norm[:, r, :], in_=v[:], func=ACT.Identity, scale=rstd[:, 0:1], bias=shift[:, 0:1]
+        for r in range(ROW_TILES):
+            v, rstd, shift = add_bias_and_measure(nc, norm_pool, x_sums[r], bias[:, 0, :], minus_half)
+            for half in range(HALVES):
+                cols = slice(half * N_TILE, (half + 1) * N_TILE)
+                both = out_pool.tile([P, N_TILE], F32, name="both")
+                nc.vector.scalar_tensor_tensor(
+                    out=both[:],
+                    in0=v[:, cols],
+                    scalar=rstd[:, 0:1],
+                    in1=h_norm[:, r, cols],
+                    op0=ALU.mult,
+                    op1=ALU.add,
                 )
-
-            x_sums = open_sums(sum_banks, "x")
-            for g in range(0, GROUPS, BLOCK):
-                multiply_groups(nc, x_sums, x_groups[g : g + BLOCK], g == 0, g + BLOCK == GROUPS)
-
-            for r in range(ROW_TILES):
-                v, rstd, shift = add_bias_and_measure(nc, norm_pool, x_sums[r], bias[:, 0, :], minus_half)
-                for half in range(HALVES):
-                    cols = slice(half * N_TILE, (half + 1) * N_TILE)
-                    both = out_pool.tile([P, N_TILE], F32, name="both")
-                    nc.vector.scalar_tensor_tensor(
-                        out=both[:],
-                        in0=v[:, cols],
-                        scalar=rstd[:, 0:1],
-                        in1=h_norm[:, r, cols],
-                        op0=ALU.mult,
-                        op1=ALU.add,
-                    )
-                    gate = out_pool.tile([P, N_TILE], F32, name="gate")
-                    nc.scalar.activation(out=gate[:], in_=both[:], func=ACT.Sigmoid, bias=shift[:, 0:1])
-                    nc.sync.dma_start(out=out[r * P : (r + 1) * P, cols], in_=gate[:])
+                gate = out_pool.tile([P, N_TILE], F32, name="gate")
+                nc.scalar.activation(out=gate[:], in_=both[:], func=ACT.Sigmoid, bias=shift[:, 0:1])
+                nc.sync.dma_start(out=out[r * P : (r + 1) * P, cols], in_=gate[:])

@@ -38,24 +38,24 @@ BLOCK_CHUNKS = BLOCK // CHUNK
 
 
 def load_scale_rows(nc, planes, scales):
-    for q in range(SCALE_ROWS // 2):
-        partition = 32 * (q // 4) + q % 4
+    for j in range(4):
         nc.sync.dma_start(
-            out=planes[partition:P:64, :, :].bitcast(I32),
-            in_=scales[:, q:SCALE_ROWS:8, :].bitcast(I32).rearrange("g q n -> q g n"),
+            out=planes[j:P:32, :, :].bitcast(I32),
+            in_=scales[:, j:SCALE_ROWS:4, :].bitcast(I32).rearrange("g q n -> q g n"),
         )
 
 
-def transpose_groups(nc, banks, raw, identity):
-    words = raw[:].bitcast(F32)
+def even_and_odd_words(raw):
+    return raw[:].bitcast(F32).rearrange("b r (g p u) -> b r g u p", p=P, u=2)
+
+
+def transpose_groups(nc, banks, words, identity):
     filled = []
-    for g in range(words.shape[2] // PAIRS):
+    for g in range(words.shape[2]):
         bank = banks.tile([P, ROW_TILES, 2, P], F32, name="bank", tag="bank")
         for r in range(ROW_TILES):
             for u in range(2):
-                nc.tensor.transpose(
-                    bank[:, r, u, :], words[:, r, g * PAIRS + u : (g + 1) * PAIRS : 2], identity[:]
-                )
+                nc.tensor.transpose(bank[:, r, u, :], words[:, r, g, u, :], identity[:])
         filled.append(bank)
     return filled
 
@@ -131,7 +131,8 @@ def tile_layernormgrucell_pa_k_kernel(
         x_pool = ctx.enter_context(tc.tile_pool(name="x", bufs=ROUND_CHUNKS))
         grouped_pool = ctx.enter_context(tc.tile_pool(name="grouped", bufs=2))
         codes_pool = ctx.enter_context(tc.tile_pool(name="codes", bufs=CHUNKS))
-        w_pool = ctx.enter_context(tc.tile_pool(name="w", bufs=CHUNKS))
+        sorted_pool = ctx.enter_context(tc.tile_pool(name="sorted", bufs=ROUND_CHUNKS))
+        w_pool = ctx.enter_context(tc.tile_pool(name="w", bufs=ROUND_CHUNKS))
         planes_pool = ctx.enter_context(tc.tile_pool(name="planes", bufs=BLOCKS))
         norm_pool = ctx.enter_context(tc.tile_pool(name="norm", bufs=2))
         out_pool = ctx.enter_context(tc.tile_pool(name="out", bufs=2))
@@ -159,6 +160,7 @@ def tile_layernormgrucell_pa_k_kernel(
 
         x_rows = x.rearrange("(r p) k -> p r k", p=P)
         x_raw = {}
+        x_words = {}
         x_groups = []
         w_groups = []
 
@@ -168,6 +170,16 @@ def tile_layernormgrucell_pa_k_kernel(
                 nc.sync.dma_start(
                     out=x_raw[c][:], in_=x_rows[:, :, c * CHUNK * K_PASS : (c + 1) * CHUNK * K_PASS]
                 )
+                x_words[c] = even_and_odd_words(x_raw[c])
+
+        def sort_x(j):
+            for c in range(j * ROUND_CHUNKS, (j + 1) * ROUND_CHUNKS):
+                sorted_words = sorted_pool.tile([P, ROW_TILES, CHUNK, 2, P], F32, name="sorted_words")
+                nc.vector.tensor_copy(
+                    out=sorted_words[:].rearrange("b r g u p -> b (r g) u p"),
+                    in_=x_words[c].rearrange("b r g u p -> b (r g) u p"),
+                )
+                x_words[c] = sorted_words[:]
 
         def load_w(j):
             load_scale_rows(nc, irz_scales[j], W_irz_scales[j * BLOCK : (j + 1) * BLOCK])
@@ -182,7 +194,7 @@ def tile_layernormgrucell_pa_k_kernel(
 
         def prepare_x(j):
             for c in range(j * ROUND_CHUNKS, (j + 1) * ROUND_CHUNKS):
-                filled = transpose_groups(nc, banks, x_raw[c], identity)
+                filled = transpose_groups(nc, banks, x_words[c], identity)
                 grouped = grouped_pool.tile([P, CHUNK, ROW_TILES, P, PACK], BF16, name="grouped", align_bytes=64)
                 x_codes = codes_pool.tile([P, CHUNK, B], U32, name="x_codes", align_bytes=64)
                 x_scales = codes_pool.tile([P, CHUNK, B], U8, name="x_scales", align_bytes=64)
@@ -220,12 +232,12 @@ def tile_layernormgrucell_pa_k_kernel(
         h_grouped = keep.tile([P, 1, ROW_TILES, P, PACK], BF16, name="h_grouped", align_bytes=64)
         h_codes = keep.tile([P, 1, B], U32, name="h_codes", align_bytes=64)
         h_scales = keep.tile([P, 1, B], U8, name="h_scales", align_bytes=64)
-        quantise_groups(nc, transpose_groups(nc, banks, h_raw, identity), h_grouped, h_codes, h_scales)
+        h_filled = transpose_groups(nc, banks, even_and_odd_words(h_raw), identity)
+        quantise_groups(nc, h_filled, h_grouped, h_codes, h_scales)
         prepare_x(0)
         load_x(1)
-        load_w(2)
-        load_w(3)
         multiply_x(0)
+        load_w(2)
 
         h_sums = [
             [banks.tile([P, N_TILE], F32, name="h_sum", tag="bank") for half in range(HALVES)]
@@ -240,7 +252,9 @@ def tile_layernormgrucell_pa_k_kernel(
                 out=h_norm[:, r, :], in_=v[:], func=ACT.Identity, scale=rstd[:, 0:1], bias=shift[:, 0:1]
             )
         multiply_x(1)
+        load_w(3)
 
+        sort_x(1)
         prepare_x(1)
         multiply_x(2)
         multiply_x(3)

@@ -101,13 +101,20 @@ def open_sums(psum, name):
     ]
 
 
-def add_bias_and_measure(nc, pool, sums_of_rows, bias, minus_half):
-    v = pool.tile([P, G], F32, name="v")
-    stats = pool.tile([P, HALVES, 6], F32, name="stats")
-    for half in range(HALVES):
-        cols = slice(half * N_TILE, (half + 1) * N_TILE)
-        nc.vector.tensor_tensor(out=v[:, cols], in0=sums_of_rows[half][:], in1=bias[:, cols], op=ALU.add)
-        nc.vector.bn_stats(out=stats[:, half, :], in_=v[:, cols])
+def half_columns(half):
+    return slice(half * N_TILE, (half + 1) * N_TILE)
+
+
+def add_bias(nc, v, sums_of_rows, bias, half):
+    cols = half_columns(half)
+    nc.vector.tensor_tensor(out=v[:, cols], in0=sums_of_rows[half][:], in1=bias[:, cols], op=ALU.add)
+
+
+def count(nc, stats, v, half):
+    nc.vector.bn_stats(out=stats[:, half, :], in_=v[:, half_columns(half)])
+
+
+def rstd_and_shift(nc, pool, stats, minus_half):
     mean_var = pool.tile([P, 2], F32, name="mean_var")
     nc.vector.bn_aggr(out=mean_var[:], in_=stats[:].rearrange("p h s -> p (h s)"))
     var_eps = pool.tile([P, 1], F32, name="var_eps")
@@ -118,7 +125,7 @@ def add_bias_and_measure(nc, pool, sums_of_rows, bias, minus_half):
     nc.vector.tensor_scalar(
         out=shift[:], in0=mean_var[:, 0:1], scalar1=rstd[:, 0:1], scalar2=-1.0, op0=ALU.mult, op1=ALU.mult
     )
-    return v, rstd, shift
+    return rstd, shift
 
 
 def tile_layernormgrucell_pa_k_kernel(
@@ -224,7 +231,7 @@ def tile_layernormgrucell_pa_k_kernel(
         bias = keep.tile([P, 2, G], F32, name="bias")
         for which in range(2):
             for half in range(HALVES):
-                cols = slice(half * N_TILE, (half + 1) * N_TILE)
+                cols = half_columns(half)
                 spread = banks.tile([P, N_TILE], F32, name="spread", tag="bank")
                 nc.tensor.matmul(out=spread[:], lhsT=ones[:], rhs=bias_rows[:, which, cols], start=True, stop=True)
                 nc.scalar.copy(out=bias[:, which, cols], in_=spread[:])
@@ -245,24 +252,38 @@ def tile_layernormgrucell_pa_k_kernel(
         ]
         h_groups = [(h_codes[:, 0, :], h_scales[:, 0, :], hrz_words[:, 0, :], hrz_scales[:, 0, :])]
         multiply_groups(nc, h_sums, h_groups, True, True)
-        h_norm = keep.tile([P, ROW_TILES, G], F32, name="h_norm")
+        h_v = []
         for r in range(ROW_TILES):
-            v, rstd, shift = add_bias_and_measure(nc, norm_pool, h_sums[r], bias[:, 1, :], minus_half)
-            nc.scalar.activation(
-                out=h_norm[:, r, :], in_=v[:], func=ACT.Identity, scale=rstd[:, 0:1], bias=shift[:, 0:1]
-            )
+            h_v.append(norm_pool.tile([P, G], F32, name="v"))
+            for half in range(HALVES):
+                add_bias(nc, h_v[r], h_sums[r], bias[:, 1, :], half)
         multiply_x(1)
         load_w(3)
 
         sort_x(1)
         prepare_x(1)
+
+        h_norm = keep.tile([P, ROW_TILES, G], F32, name="h_norm")
+        for r in range(ROW_TILES):
+            stats = norm_pool.tile([P, HALVES, 6], F32, name="stats")
+            for half in range(HALVES):
+                count(nc, stats, h_v[r], half)
+            rstd, shift = rstd_and_shift(nc, norm_pool, stats, minus_half)
+            nc.scalar.activation(
+                out=h_norm[:, r, :], in_=h_v[r][:], func=ACT.Identity, scale=rstd[:, 0:1], bias=shift[:, 0:1]
+            )
         multiply_x(2)
         multiply_x(3)
 
         for r in range(ROW_TILES):
-            v, rstd, shift = add_bias_and_measure(nc, norm_pool, x_sums[r], bias[:, 0, :], minus_half)
+            v = norm_pool.tile([P, G], F32, name="v")
+            stats = norm_pool.tile([P, HALVES, 6], F32, name="stats")
             for half in range(HALVES):
-                cols = slice(half * N_TILE, (half + 1) * N_TILE)
+                add_bias(nc, v, x_sums[r], bias[:, 0, :], half)
+                count(nc, stats, v, half)
+            rstd, shift = rstd_and_shift(nc, norm_pool, stats, minus_half)
+            for half in range(HALVES):
+                cols = half_columns(half)
                 both = out_pool.tile([P, N_TILE], F32, name="both")
                 nc.vector.scalar_tensor_tensor(
                     out=both[:],

@@ -20,7 +20,6 @@ FLOPS = 2 * B * (I + H) * G
 P = 128
 PACK = 4
 K_PASS = P * PACK
-PAIRS = K_PASS // 2
 ROW_TILES = B // P
 N_TILE = 512
 HALVES = G // N_TILE
@@ -29,12 +28,10 @@ GROUPS = I // K_PASS
 
 CHUNK = 4
 CHUNKS = GROUPS // CHUNK
-ROUNDS = 2
-ROUND_CHUNKS = CHUNKS // ROUNDS
-SCALAR_BANKS = 3
-BLOCK = 8
-BLOCKS = GROUPS // BLOCK
-BLOCK_CHUNKS = BLOCK // CHUNK
+AHEAD = 2
+X_BUFS = AHEAD + 1
+SCALAR_BANKS = 2
+LAST_CHUNKS = 2
 
 
 def load_scale_rows(nc, planes, scales):
@@ -60,7 +57,7 @@ def transpose_groups(nc, banks, words, identity):
     return filled
 
 
-def quantise_groups(nc, filled, grouped, codes, scales):
+def empty_banks(nc, filled, grouped):
     for g, bank in enumerate(filled):
         side_by_side = grouped[:, g].bitcast(F32)
         alternately = bank[:].rearrange("p r u b -> p r b u")
@@ -68,6 +65,9 @@ def quantise_groups(nc, filled, grouped, codes, scales):
             nc.scalar.copy(out=side_by_side, in_=alternately)
         else:
             nc.vector.tensor_copy(out=side_by_side, in_=alternately)
+
+
+def quantise(nc, grouped, codes, scales):
     nc.vector.quantize_mx(
         out=codes[:].rearrange("p g c -> p (g c)").bitcast(FP8X4),
         scales=scales[:].rearrange("p g c -> p (g c)"),
@@ -75,30 +75,18 @@ def quantise_groups(nc, filled, grouped, codes, scales):
     )
 
 
-def multiply_groups(nc, sums, groups, first, last):
-    for r in range(ROW_TILES):
-        rows = slice(r * P, (r + 1) * P)
-        for half in range(HALVES):
-            for i, (codes, scales, w_words, w_scales) in enumerate(groups):
-                nc.tensor.matmul_mx(
-                    out=sums[r][half][:],
-                    lhsT=codes[:, rows].bitcast(FP8X4),
-                    lhsT_scale=scales[:, rows],
-                    rhs=w_words[:, half * 2 * N_TILE : (half + 1) * 2 * N_TILE].bitcast(FP4X4),
-                    rhs_scale=w_scales[:, half * N_TILE : (half + 1) * N_TILE],
-                    start=first and i == 0,
-                    stop=last and i == len(groups) - 1,
-                )
-
-
-def open_sums(psum, name):
-    return [
-        [
-            psum.tile([P, N_TILE], F32, name="%s%d%d" % (name, r, half), tag="%s%d%d" % (name, r, half))
-            for half in range(HALVES)
-        ]
-        for r in range(ROW_TILES)
-    ]
+def multiply_groups(nc, total, r, half, groups, first, last):
+    rows = slice(r * P, (r + 1) * P)
+    for i, (codes, scales, w_words, w_scales) in enumerate(groups):
+        nc.tensor.matmul_mx(
+            out=total[:],
+            lhsT=codes[:, rows].bitcast(FP8X4),
+            lhsT_scale=scales[:, rows],
+            rhs=w_words[:, half * 2 * N_TILE : (half + 1) * 2 * N_TILE].bitcast(FP4X4),
+            rhs_scale=w_scales[:, half * N_TILE : (half + 1) * N_TILE],
+            start=first and i == 0,
+            stop=last and i == len(groups) - 1,
+        )
 
 
 def half_columns(half):
@@ -135,19 +123,88 @@ def tile_layernormgrucell_pa_k_kernel(
     with ExitStack() as ctx:
         ctx.enter_context(tc.manual_schedule())
         keep = ctx.enter_context(tc.tile_pool(name="keep", bufs=1))
-        x_pool = ctx.enter_context(tc.tile_pool(name="x", bufs=ROUND_CHUNKS))
+        x_pool = ctx.enter_context(tc.tile_pool(name="x", bufs=X_BUFS))
+        sorted_pool = ctx.enter_context(tc.tile_pool(name="sorted", bufs=2))
         grouped_pool = ctx.enter_context(tc.tile_pool(name="grouped", bufs=2))
-        codes_pool = ctx.enter_context(tc.tile_pool(name="codes", bufs=CHUNKS))
-        sorted_pool = ctx.enter_context(tc.tile_pool(name="sorted", bufs=ROUND_CHUNKS))
-        w_pool = ctx.enter_context(tc.tile_pool(name="w", bufs=ROUND_CHUNKS))
-        planes_pool = ctx.enter_context(tc.tile_pool(name="planes", bufs=BLOCKS))
+        codes_pool = ctx.enter_context(tc.tile_pool(name="codes", bufs=AHEAD + 2))
+        w_pool = ctx.enter_context(tc.tile_pool(name="w", bufs=CHUNKS))
         norm_pool = ctx.enter_context(tc.tile_pool(name="norm", bufs=2))
         out_pool = ctx.enter_context(tc.tile_pool(name="out", bufs=2))
         sum_banks = ctx.enter_context(tc.psum_pool(name="sums", bufs=1))
         banks = ctx.enter_context(tc.psum_pool(name="banks", bufs=4))
 
+        x_rows = x.rearrange("(r p) k -> p r k", p=P)
+        x_raw = {}
+        x_words = {}
+        x_groups = []
+        w_groups = []
+        irz_scales = {}
+
+        def load_x(c):
+            x_raw[c] = x_pool.tile([P, ROW_TILES, CHUNK * K_PASS], BF16, name="x_raw")
+            nc.sync.dma_start(out=x_raw[c][:], in_=x_rows[:, :, c * CHUNK * K_PASS : (c + 1) * CHUNK * K_PASS])
+
+        def zero_scales(c):
+            irz_scales[c] = w_pool.tile([P, CHUNK, G], U8, name="irz_scales", align_bytes=64)
+            nc.vector.memset(irz_scales[c][:].bitcast(I32), 0)
+
+        def load_w(c):
+            load_scale_rows(nc, irz_scales[c], W_irz_scales[c * CHUNK : (c + 1) * CHUNK])
+            w_words = w_pool.tile([P, CHUNK, 2 * G], U8, name="w_words", align_bytes=64)
+            nc.sync.dma_start(
+                out=w_words[:].bitcast(I32),
+                in_=W_irz_words[c * CHUNK : (c + 1) * CHUNK].bitcast(I32).rearrange("g p n -> p g n"),
+            )
+            for g in range(CHUNK):
+                w_groups.append((w_words[:, g, :], irz_scales[c][:, g, :]))
+
+        def sort_x(c, copy):
+            sorted_words = sorted_pool.tile([P, ROW_TILES, CHUNK, 2, P], F32, name="sorted_words")
+            copy(
+                out=sorted_words[:].rearrange("b r g u p -> b (r g) u p"),
+                in_=even_and_odd_words(x_raw[c]).rearrange("b r g u p -> b (r g) u p"),
+            )
+            x_words[c] = sorted_words[:]
+
+        def turn_x(c):
+            filled = transpose_groups(nc, banks, x_words[c], identity)
+            grouped = grouped_pool.tile([P, CHUNK, ROW_TILES, P, PACK], BF16, name="grouped", align_bytes=64)
+            x_codes = codes_pool.tile([P, CHUNK, B], U32, name="x_codes", align_bytes=64)
+            x_scales = codes_pool.tile([P, CHUNK, B], U8, name="x_scales", align_bytes=64)
+            empty_banks(nc, filled, grouped)
+            quantise(nc, grouped, x_codes, x_scales)
+            for g in range(CHUNK):
+                x_groups.append((x_codes[:, g, :], x_scales[:, g, :]))
+
+        def load_behind(c):
+            if c + AHEAD < CHUNKS:
+                zero_scales(c + AHEAD)
+            if c + X_BUFS < CHUNKS:
+                load_x(c + X_BUFS)
+            if c + AHEAD < CHUNKS:
+                load_w(c + AHEAD)
+
+        x_sums = [
+            [sum_banks.tile([P, N_TILE], F32, name="x%d%d" % (r, half), tag="x%d%d" % (r, half)) for half in range(HALVES)]
+            for r in range(ROW_TILES)
+        ]
+
+        def multiply_x(r, half, chunks):
+            some = [g for c in chunks for g in range(c * CHUNK, (c + 1) * CHUNK)]
+            multiply_groups(
+                nc, x_sums[r][half], r, half, [x_groups[g] + w_groups[g] for g in some], some[0] == 0, some[-1] == GROUPS - 1
+            )
+
+        load_x(0)
         bias_rows = keep.tile([P, 2, G], BF16, name="bias_rows")
-        nc.vector.memset(bias_rows[:], 0.0)
+        nc.vector.memset(bias_rows[:].rearrange("p w n -> p (w n)").bitcast(F32), 0.0)
+        nc.sync.dma_start(out=bias_rows[0:1, 0, :], in_=b_irz.rearrange("(o n) -> o n", o=1))
+        nc.sync.dma_start(out=bias_rows[0:1, 1, :], in_=b_hrz.rearrange("(o n) -> o n", o=1))
+        h_raw = keep.tile([P, ROW_TILES, H], BF16, name="h_raw")
+        nc.sync.dma_start(out=h_raw[:], in_=h.rearrange("(r p) k -> p r k", p=P))
+        load_x(1)
+        zero_scales(0)
+        load_w(0)
         ones = keep.tile([P, P], BF16, name="ones")
         nc.vector.memset(ones[:], 1.0)
         minus_half = keep.tile([P, 1], F32, name="minus_half")
@@ -158,74 +215,13 @@ def tile_layernormgrucell_pa_k_kernel(
         make_identity(nc, identity[:])
         warm = keep.tile([P, 1], F32, name="warm")
         nc.scalar.activation(out=warm[:], in_=zero[:], func=ACT.Sigmoid)
-        irz_scales = []
-        for j in range(BLOCKS):
-            irz_scales.append(planes_pool.tile([P, BLOCK, G], U8, name="irz_scales", align_bytes=64))
-            nc.vector.memset(irz_scales[j][:].bitcast(I32), 0)
         hrz_scales = keep.tile([P, 1, G], U8, name="hrz_scales", align_bytes=64)
         nc.vector.memset(hrz_scales[:].bitcast(I32), 0)
-
-        x_rows = x.rearrange("(r p) k -> p r k", p=P)
-        x_raw = {}
-        x_words = {}
-        x_groups = []
-        w_groups = []
-
-        def load_x(j):
-            for c in range(j * ROUND_CHUNKS, (j + 1) * ROUND_CHUNKS):
-                x_raw[c] = x_pool.tile([P, ROW_TILES, CHUNK * K_PASS], BF16, name="x_raw")
-                nc.sync.dma_start(
-                    out=x_raw[c][:], in_=x_rows[:, :, c * CHUNK * K_PASS : (c + 1) * CHUNK * K_PASS]
-                )
-                x_words[c] = even_and_odd_words(x_raw[c])
-
-        def sort_x(j):
-            for c in range(j * ROUND_CHUNKS, (j + 1) * ROUND_CHUNKS):
-                sorted_words = sorted_pool.tile([P, ROW_TILES, CHUNK, 2, P], F32, name="sorted_words")
-                nc.vector.tensor_copy(
-                    out=sorted_words[:].rearrange("b r g u p -> b (r g) u p"),
-                    in_=x_words[c].rearrange("b r g u p -> b (r g) u p"),
-                )
-                x_words[c] = sorted_words[:]
-
-        def load_w(j):
-            load_scale_rows(nc, irz_scales[j], W_irz_scales[j * BLOCK : (j + 1) * BLOCK])
-            for c in range(j * BLOCK_CHUNKS, (j + 1) * BLOCK_CHUNKS):
-                w_words = w_pool.tile([P, CHUNK, 2 * G], U8, name="w_words", align_bytes=64)
-                nc.sync.dma_start(
-                    out=w_words[:].bitcast(I32),
-                    in_=W_irz_words[c * CHUNK : (c + 1) * CHUNK].bitcast(I32).rearrange("g p n -> p g n"),
-                )
-                for g in range(CHUNK):
-                    w_groups.append((w_words[:, g, :], irz_scales[j][:, (c * CHUNK + g) % BLOCK, :]))
-
-        def prepare_x(j):
-            for c in range(j * ROUND_CHUNKS, (j + 1) * ROUND_CHUNKS):
-                filled = transpose_groups(nc, banks, x_words[c], identity)
-                grouped = grouped_pool.tile([P, CHUNK, ROW_TILES, P, PACK], BF16, name="grouped", align_bytes=64)
-                x_codes = codes_pool.tile([P, CHUNK, B], U32, name="x_codes", align_bytes=64)
-                x_scales = codes_pool.tile([P, CHUNK, B], U8, name="x_scales", align_bytes=64)
-                quantise_groups(nc, filled, grouped, x_codes, x_scales)
-                for g in range(CHUNK):
-                    x_groups.append((x_codes[:, g, :], x_scales[:, g, :]))
-
-        x_sums = open_sums(sum_banks, "x")
-
-        def multiply_x(j):
-            some = range(j * BLOCK, (j + 1) * BLOCK)
-            multiply_groups(nc, x_sums, [x_groups[g] + w_groups[g] for g in some], j == 0, j == BLOCKS - 1)
-
-        nc.sync.dma_start(out=bias_rows[0:1, 0, :], in_=b_irz.rearrange("(o n) -> o n", o=1))
-        nc.sync.dma_start(out=bias_rows[0:1, 1, :], in_=b_hrz.rearrange("(o n) -> o n", o=1))
-        h_raw = keep.tile([P, ROW_TILES, H], BF16, name="h_raw")
-        nc.sync.dma_start(out=h_raw[:], in_=h.rearrange("(r p) k -> p r k", p=P))
-        load_x(0)
-        load_w(0)
         load_scale_rows(nc, hrz_scales, W_hrz_scales)
         hrz_words = keep.tile([P, 1, 2 * G], U8, name="hrz_words", align_bytes=64)
-        nc.sync.dma_start(
-            out=hrz_words[:].bitcast(I32), in_=W_hrz_words.bitcast(I32).rearrange("g p n -> p g n")
-        )
+        nc.sync.dma_start(out=hrz_words[:].bitcast(I32), in_=W_hrz_words.bitcast(I32).rearrange("g p n -> p g n"))
+        load_x(AHEAD)
+        zero_scales(1)
         load_w(1)
 
         bias = keep.tile([P, 2, G], F32, name="bias")
@@ -239,41 +235,54 @@ def tile_layernormgrucell_pa_k_kernel(
         h_grouped = keep.tile([P, 1, ROW_TILES, P, PACK], BF16, name="h_grouped", align_bytes=64)
         h_codes = keep.tile([P, 1, B], U32, name="h_codes", align_bytes=64)
         h_scales = keep.tile([P, 1, B], U8, name="h_scales", align_bytes=64)
-        h_filled = transpose_groups(nc, banks, even_and_odd_words(h_raw), identity)
-        quantise_groups(nc, h_filled, h_grouped, h_codes, h_scales)
-        prepare_x(0)
-        load_x(1)
-        multiply_x(0)
-        load_w(2)
+        empty_banks(nc, transpose_groups(nc, banks, even_and_odd_words(h_raw), identity), h_grouped)
+        for c in range(AHEAD):
+            sort_x(c, nc.vector.tensor_copy)
+        for c in range(AHEAD):
+            turn_x(c)
+            load_behind(c)
+        quantise(nc, h_grouped, h_codes, h_scales)
 
-        h_sums = [
-            [banks.tile([P, N_TILE], F32, name="h_sum", tag="bank") for half in range(HALVES)]
-            for r in range(ROW_TILES)
-        ]
-        h_groups = [(h_codes[:, 0, :], h_scales[:, 0, :], hrz_words[:, 0, :], hrz_scales[:, 0, :])]
-        multiply_groups(nc, h_sums, h_groups, True, True)
         h_v = []
-        for r in range(ROW_TILES):
-            h_v.append(norm_pool.tile([P, G], F32, name="v"))
-            for half in range(HALVES):
-                add_bias(nc, h_v[r], h_sums[r], bias[:, 1, :], half)
-        multiply_x(1)
-        load_w(3)
 
-        sort_x(1)
-        prepare_x(1)
+        def multiply_h():
+            h_groups = [(h_codes[:, 0, :], h_scales[:, 0, :], hrz_words[:, 0, :], hrz_scales[:, 0, :])]
+            for r in range(ROW_TILES):
+                h_v.append(norm_pool.tile([P, G], F32, name="v"))
+                h_sums = []
+                for half in range(HALVES):
+                    h_sums.append(banks.tile([P, N_TILE], F32, name="h_sum", tag="bank"))
+                    multiply_groups(nc, h_sums[half], r, half, h_groups, True, True)
+                    add_bias(nc, h_v[r], h_sums, bias[:, 1, :], half)
 
         h_norm = keep.tile([P, ROW_TILES, G], F32, name="h_norm")
-        for r in range(ROW_TILES):
+
+        def normalise_h(r):
             stats = norm_pool.tile([P, HALVES, 6], F32, name="stats")
             for half in range(HALVES):
                 count(nc, stats, h_v[r], half)
             rstd, shift = rstd_and_shift(nc, norm_pool, stats, minus_half)
-            nc.scalar.activation(
-                out=h_norm[:, r, :], in_=h_v[r][:], func=ACT.Identity, scale=rstd[:, 0:1], bias=shift[:, 0:1]
+            nc.vector.tensor_scalar(
+                out=h_norm[:, r, :], in0=h_v[r][:], scalar1=rstd[:, 0:1], scalar2=shift[:, 0:1], op0=ALU.mult, op1=ALU.add
             )
-        multiply_x(2)
-        multiply_x(3)
+
+        for c in range(CHUNKS - LAST_CHUNKS):
+            for r in range(ROW_TILES):
+                for half in range(HALVES):
+                    multiply_x(r, half, [c])
+                if c == 0 and r == 0:
+                    multiply_h()
+            sort_x(c + AHEAD, nc.scalar.copy)
+            turn_x(c + AHEAD)
+            load_behind(c + AHEAD)
+            if c < ROW_TILES:
+                normalise_h(c)
+        last = list(range(CHUNKS - LAST_CHUNKS, CHUNKS))
+        for c in last:
+            for half in range(HALVES):
+                multiply_x(0, half, [c])
+        for half in range(HALVES):
+            multiply_x(1, half, last)
 
         for r in range(ROW_TILES):
             v = norm_pool.tile([P, G], F32, name="v")

@@ -110,7 +110,7 @@ def rstd_and_shift(nc, pool, stats, minus_half):
     rstd = pool.tile([P, 1], F32, name="rstd")
     nc.gpsimd.tensor_tensor(out=rstd[:], in0=var_eps[:], in1=minus_half[:], op=ALU.pow)
     shift = pool.tile([P, 1], F32, name="shift")
-    nc.vector.tensor_scalar(
+    nc.gpsimd.tensor_scalar(
         out=shift[:], in0=mean_var[:, 0:1], scalar1=rstd[:, 0:1], scalar2=-1.0, op0=ALU.mult, op1=ALU.mult
     )
     return rstd, shift
@@ -130,6 +130,7 @@ def tile_layernormgrucell_pa_k_kernel(
         w_pool = ctx.enter_context(tc.tile_pool(name="w", bufs=CHUNKS))
         norm_pool = ctx.enter_context(tc.tile_pool(name="norm", bufs=2))
         out_pool = ctx.enter_context(tc.tile_pool(name="out", bufs=2))
+        gate_pool = ctx.enter_context(tc.tile_pool(name="gate", bufs=ROW_TILES * HALVES))
         sum_banks = ctx.enter_context(tc.psum_pool(name="sums", bufs=1))
         banks = ctx.enter_context(tc.psum_pool(name="banks", bufs=4))
 
@@ -240,8 +241,9 @@ def tile_layernormgrucell_pa_k_kernel(
             sort_x(c, nc.vector.tensor_copy)
         for c in range(AHEAD):
             turn_x(c)
+            if c == 0:
+                quantise(nc, h_grouped, h_codes, h_scales)
             load_behind(c)
-        quantise(nc, h_grouped, h_codes, h_scales)
 
         h_v = []
 
@@ -284,24 +286,34 @@ def tile_layernormgrucell_pa_k_kernel(
         for half in range(HALVES):
             multiply_x(1, half, last)
 
-        for r in range(ROW_TILES):
-            v = norm_pool.tile([P, G], F32, name="v")
-            stats = norm_pool.tile([P, HALVES, 6], F32, name="stats")
-            for half in range(HALVES):
-                add_bias(nc, v, x_sums[r], bias[:, 0, :], half)
-                count(nc, stats, v, half)
-            rstd, shift = rstd_and_shift(nc, norm_pool, stats, minus_half)
+        x_v = [norm_pool.tile([P, G], F32, name="v") for r in range(ROW_TILES)]
+        x_stats = [norm_pool.tile([P, HALVES, 6], F32, name="stats") for r in range(ROW_TILES)]
+
+        def take(r, half):
+            add_bias(nc, x_v[r], x_sums[r], bias[:, 0, :], half)
+            count(nc, x_stats[r], x_v[r], half)
+
+        def finish(r, rstd, shift):
             for half in range(HALVES):
                 cols = half_columns(half)
                 both = out_pool.tile([P, N_TILE], F32, name="both")
                 nc.vector.scalar_tensor_tensor(
                     out=both[:],
-                    in0=v[:, cols],
+                    in0=x_v[r][:, cols],
                     scalar=rstd[:, 0:1],
                     in1=h_norm[:, r, cols],
                     op0=ALU.mult,
                     op1=ALU.add,
                 )
-                gate = out_pool.tile([P, N_TILE], F32, name="gate")
+                gate = gate_pool.tile([P, N_TILE], F32, name="gate")
                 nc.scalar.activation(out=gate[:], in_=both[:], func=ACT.Sigmoid, bias=shift[:, 0:1])
                 nc.sync.dma_start(out=out[r * P : (r + 1) * P, cols], in_=gate[:])
+
+        take(0, 0)
+        take(0, 1)
+        rstd_0, shift_0 = rstd_and_shift(nc, norm_pool, x_stats[0], minus_half)
+        take(1, 0)
+        finish(0, rstd_0, shift_0)
+        take(1, 1)
+        rstd_1, shift_1 = rstd_and_shift(nc, norm_pool, x_stats[1], minus_half)
+        finish(1, rstd_1, shift_1)

@@ -26,11 +26,13 @@ HALVES = G // N_TILE
 SCALE_ROWS = K_PASS // 32
 GROUPS = I // K_PASS
 
-CHUNK = 4
-CHUNKS = GROUPS // CHUNK
+CHUNK_GROUPS = [4, 4, 4, 4, 4, 4, 4, 4]
+CHUNKS = len(CHUNK_GROUPS)
+CHUNK_START = [sum(CHUNK_GROUPS[:c]) for c in range(CHUNKS)]
 AHEAD = 2
 X_BUFS = AHEAD + 1
 SCALAR_BANKS = 2
+SCALE_CHUNKS = 2
 LAST_CHUNKS = 2
 
 
@@ -61,7 +63,7 @@ def empty_banks(nc, filled, grouped):
     for g, bank in enumerate(filled):
         side_by_side = grouped[:, g].bitcast(F32)
         alternately = bank[:].rearrange("p r u b -> p r b u")
-        if g < SCALAR_BANKS:
+        if g % 4 < SCALAR_BANKS:
             nc.scalar.copy(out=side_by_side, in_=alternately)
         else:
             nc.vector.tensor_copy(out=side_by_side, in_=alternately)
@@ -127,7 +129,6 @@ def tile_layernormgrucell_pa_k_kernel(
         sorted_pool = ctx.enter_context(tc.tile_pool(name="sorted", bufs=2))
         grouped_pool = ctx.enter_context(tc.tile_pool(name="grouped", bufs=2))
         codes_pool = ctx.enter_context(tc.tile_pool(name="codes", bufs=AHEAD + 2))
-        w_pool = ctx.enter_context(tc.tile_pool(name="w", bufs=CHUNKS))
         norm_pool = ctx.enter_context(tc.tile_pool(name="norm", bufs=2))
         out_pool = ctx.enter_context(tc.tile_pool(name="out", bufs=2))
         gate_pool = ctx.enter_context(tc.tile_pool(name="gate", bufs=ROW_TILES * HALVES))
@@ -142,25 +143,31 @@ def tile_layernormgrucell_pa_k_kernel(
         irz_scales = {}
 
         def load_x(c):
-            x_raw[c] = x_pool.tile([P, ROW_TILES, CHUNK * K_PASS], BF16, name="x_raw")
-            nc.sync.dma_start(out=x_raw[c][:], in_=x_rows[:, :, c * CHUNK * K_PASS : (c + 1) * CHUNK * K_PASS])
+            x_raw[c] = x_pool.tile([P, ROW_TILES, CHUNK_GROUPS[c] * K_PASS], BF16, name="x_raw")
+            first_k = CHUNK_START[c] * K_PASS
+            nc.sync.dma_start(out=x_raw[c][:], in_=x_rows[:, :, first_k : first_k + CHUNK_GROUPS[c] * K_PASS])
 
         def zero_scales(c):
-            irz_scales[c] = w_pool.tile([P, CHUNK, G], U8, name="irz_scales", align_bytes=64)
-            nc.vector.memset(irz_scales[c][:].bitcast(I32), 0)
+            if c % SCALE_CHUNKS == 0:
+                groups = sum(CHUNK_GROUPS[c : c + SCALE_CHUNKS])
+                irz_scales[c] = keep.tile([P, groups, G], U8, name="irz_scales%d" % c, align_bytes=64)
+                nc.vector.memset(irz_scales[c][:].bitcast(I32), 0)
 
         def load_w(c):
-            load_scale_rows(nc, irz_scales[c], W_irz_scales[c * CHUNK : (c + 1) * CHUNK])
-            w_words = w_pool.tile([P, CHUNK, 2 * G], U8, name="w_words", align_bytes=64)
+            some = slice(CHUNK_START[c], CHUNK_START[c] + CHUNK_GROUPS[c])
+            first = c - c % SCALE_CHUNKS
+            if c == first:
+                groups = sum(CHUNK_GROUPS[c : c + SCALE_CHUNKS])
+                load_scale_rows(nc, irz_scales[c], W_irz_scales[CHUNK_START[c] : CHUNK_START[c] + groups])
+            w_words = keep.tile([P, CHUNK_GROUPS[c], 2 * G], U8, name="w_words%d" % c, align_bytes=64)
             nc.sync.dma_start(
-                out=w_words[:].bitcast(I32),
-                in_=W_irz_words[c * CHUNK : (c + 1) * CHUNK].bitcast(I32).rearrange("g p n -> p g n"),
+                out=w_words[:].bitcast(I32), in_=W_irz_words[some].bitcast(I32).rearrange("g p n -> p g n")
             )
-            for g in range(CHUNK):
-                w_groups.append((w_words[:, g, :], irz_scales[c][:, g, :]))
+            for g in range(CHUNK_GROUPS[c]):
+                w_groups.append((w_words[:, g, :], irz_scales[first][:, CHUNK_START[c] - CHUNK_START[first] + g, :]))
 
         def sort_x(c, copy):
-            sorted_words = sorted_pool.tile([P, ROW_TILES, CHUNK, 2, P], F32, name="sorted_words")
+            sorted_words = sorted_pool.tile([P, ROW_TILES, CHUNK_GROUPS[c], 2, P], F32, name="sorted_words")
             copy(
                 out=sorted_words[:].rearrange("b r g u p -> b (r g) u p"),
                 in_=even_and_odd_words(x_raw[c]).rearrange("b r g u p -> b (r g) u p"),
@@ -169,12 +176,12 @@ def tile_layernormgrucell_pa_k_kernel(
 
         def turn_x(c):
             filled = transpose_groups(nc, banks, x_words[c], identity)
-            grouped = grouped_pool.tile([P, CHUNK, ROW_TILES, P, PACK], BF16, name="grouped", align_bytes=64)
-            x_codes = codes_pool.tile([P, CHUNK, B], U32, name="x_codes", align_bytes=64)
-            x_scales = codes_pool.tile([P, CHUNK, B], U8, name="x_scales", align_bytes=64)
+            grouped = grouped_pool.tile([P, CHUNK_GROUPS[c], ROW_TILES, P, PACK], BF16, name="grouped", align_bytes=64)
+            x_codes = codes_pool.tile([P, CHUNK_GROUPS[c], B], U32, name="x_codes", align_bytes=64)
+            x_scales = codes_pool.tile([P, CHUNK_GROUPS[c], B], U8, name="x_scales", align_bytes=64)
             empty_banks(nc, filled, grouped)
             quantise(nc, grouped, x_codes, x_scales)
-            for g in range(CHUNK):
+            for g in range(CHUNK_GROUPS[c]):
                 x_groups.append((x_codes[:, g, :], x_scales[:, g, :]))
 
         def load_behind(c):
@@ -191,7 +198,7 @@ def tile_layernormgrucell_pa_k_kernel(
         ]
 
         def multiply_x(r, half, chunks):
-            some = [g for c in chunks for g in range(c * CHUNK, (c + 1) * CHUNK)]
+            some = [g for c in chunks for g in range(CHUNK_START[c], CHUNK_START[c] + CHUNK_GROUPS[c])]
             multiply_groups(
                 nc, x_sums[r][half], r, half, [x_groups[g] + w_groups[g] for g in some], some[0] == 0, some[-1] == GROUPS - 1
             )
@@ -268,21 +275,20 @@ def tile_layernormgrucell_pa_k_kernel(
                 out=h_norm[:, r, :], in0=h_v[r][:], scalar1=rstd[:, 0:1], scalar2=shift[:, 0:1], op0=ALU.mult, op1=ALU.add
             )
 
-        for c in range(CHUNKS - LAST_CHUNKS):
+        last = list(range(CHUNKS - LAST_CHUNKS, CHUNKS))
+        for c in range(CHUNKS):
             for r in range(ROW_TILES):
-                for half in range(HALVES):
-                    multiply_x(r, half, [c])
+                if r == 0 or c not in last:
+                    for half in range(HALVES):
+                        multiply_x(r, half, [c])
                 if c == 0 and r == 0:
                     multiply_h()
-            sort_x(c + AHEAD, nc.scalar.copy)
-            turn_x(c + AHEAD)
-            load_behind(c + AHEAD)
+            if c + AHEAD < CHUNKS:
+                sort_x(c + AHEAD, nc.scalar.copy)
+                turn_x(c + AHEAD)
+                load_behind(c + AHEAD)
             if c < ROW_TILES:
                 normalise_h(c)
-        last = list(range(CHUNKS - LAST_CHUNKS, CHUNKS))
-        for c in last:
-            for half in range(HALVES):
-                multiply_x(0, half, [c])
         for half in range(HALVES):
             multiply_x(1, half, last)
 

@@ -32,7 +32,6 @@ CHUNK_START = [sum(CHUNK_GROUPS[:c]) for c in range(CHUNKS)]
 AHEAD = 2
 X_BUFS = AHEAD + 1
 SCALAR_BANKS = 2
-SCALE_CHUNKS = 2
 LAST_CHUNKS = 2
 
 
@@ -148,23 +147,18 @@ def tile_layernormgrucell_pa_k_kernel(
             nc.sync.dma_start(out=x_raw[c][:], in_=x_rows[:, :, first_k : first_k + CHUNK_GROUPS[c] * K_PASS])
 
         def zero_scales(c):
-            if c % SCALE_CHUNKS == 0:
-                groups = sum(CHUNK_GROUPS[c : c + SCALE_CHUNKS])
-                irz_scales[c] = keep.tile([P, groups, G], U8, name="irz_scales%d" % c, align_bytes=64)
-                nc.vector.memset(irz_scales[c][:].bitcast(I32), 0)
+            irz_scales[c] = keep.tile([P, CHUNK_GROUPS[c], G], U8, name="irz_scales%d" % c, align_bytes=64)
+            nc.vector.memset(irz_scales[c][:].bitcast(I32), 0)
 
         def load_w(c):
             some = slice(CHUNK_START[c], CHUNK_START[c] + CHUNK_GROUPS[c])
-            first = c - c % SCALE_CHUNKS
-            if c == first:
-                groups = sum(CHUNK_GROUPS[c : c + SCALE_CHUNKS])
-                load_scale_rows(nc, irz_scales[c], W_irz_scales[CHUNK_START[c] : CHUNK_START[c] + groups])
+            load_scale_rows(nc, irz_scales[c], W_irz_scales[some])
             w_words = keep.tile([P, CHUNK_GROUPS[c], 2 * G], U8, name="w_words%d" % c, align_bytes=64)
             nc.sync.dma_start(
                 out=w_words[:].bitcast(I32), in_=W_irz_words[some].bitcast(I32).rearrange("g p n -> p g n")
             )
             for g in range(CHUNK_GROUPS[c]):
-                w_groups.append((w_words[:, g, :], irz_scales[first][:, CHUNK_START[c] - CHUNK_START[first] + g, :]))
+                w_groups.append((w_words[:, g, :], irz_scales[c][:, g, :]))
 
         def sort_x(c, copy):
             sorted_words = sorted_pool.tile([P, ROW_TILES, CHUNK_GROUPS[c], 2, P], F32, name="sorted_words")

@@ -147,13 +147,13 @@ def tile_layernormgrucell_pa_k_kernel(
             nc.sync.dma_start(out=x_raw[c][:], in_=x_rows[:, :, first_k : first_k + CHUNK_GROUPS[c] * K_PASS])
 
         def zero_scales(c):
-            irz_scales[c] = keep.tile([P, CHUNK_GROUPS[c], G], U8, name="irz_scales%d" % c, align_bytes=64)
+            irz_scales[c] = keep.tile([P, CHUNK_GROUPS[c], G], U8, name="irz_scales%d" % c, align_bytes=256)
             nc.vector.memset(irz_scales[c][:].bitcast(I32), 0)
 
         def load_w(c):
             some = slice(CHUNK_START[c], CHUNK_START[c] + CHUNK_GROUPS[c])
             load_scale_rows(nc, irz_scales[c], W_irz_scales[some])
-            w_words = keep.tile([P, CHUNK_GROUPS[c], 2 * G], U8, name="w_words%d" % c, align_bytes=64)
+            w_words = keep.tile([P, CHUNK_GROUPS[c], 2 * G], U8, name="w_words%d" % c, align_bytes=256)
             nc.sync.dma_start(
                 out=w_words[:].bitcast(I32), in_=W_irz_words[some].bitcast(I32).rearrange("g p n -> p g n")
             )
@@ -170,9 +170,9 @@ def tile_layernormgrucell_pa_k_kernel(
 
         def turn_x(c):
             filled = transpose_groups(nc, banks, x_words[c], identity)
-            grouped = grouped_pool.tile([P, CHUNK_GROUPS[c], ROW_TILES, P, PACK], BF16, name="grouped", align_bytes=64)
-            x_codes = codes_pool.tile([P, CHUNK_GROUPS[c], B], U32, name="x_codes", align_bytes=64)
-            x_scales = codes_pool.tile([P, CHUNK_GROUPS[c], B], U8, name="x_scales", align_bytes=64)
+            grouped = grouped_pool.tile([P, CHUNK_GROUPS[c], ROW_TILES, P, PACK], BF16, name="grouped", align_bytes=256)
+            x_codes = codes_pool.tile([P, CHUNK_GROUPS[c], B], U32, name="x_codes", align_bytes=256)
+            x_scales = codes_pool.tile([P, CHUNK_GROUPS[c], B], U8, name="x_scales", align_bytes=256)
             empty_banks(nc, filled, grouped)
             quantise(nc, grouped, x_codes, x_scales)
             for g in range(CHUNK_GROUPS[c]):
@@ -217,10 +217,10 @@ def tile_layernormgrucell_pa_k_kernel(
         make_identity(nc, identity[:])
         warm = keep.tile([P, 1], F32, name="warm")
         nc.scalar.activation(out=warm[:], in_=zero[:], func=ACT.Sigmoid)
-        hrz_scales = keep.tile([P, 1, G], U8, name="hrz_scales", align_bytes=64)
+        hrz_scales = keep.tile([P, 1, G], U8, name="hrz_scales", align_bytes=256)
         nc.vector.memset(hrz_scales[:].bitcast(I32), 0)
         load_scale_rows(nc, hrz_scales, W_hrz_scales)
-        hrz_words = keep.tile([P, 1, 2 * G], U8, name="hrz_words", align_bytes=64)
+        hrz_words = keep.tile([P, 1, 2 * G], U8, name="hrz_words", align_bytes=256)
         nc.sync.dma_start(out=hrz_words[:].bitcast(I32), in_=W_hrz_words.bitcast(I32).rearrange("g p n -> p g n"))
         load_x(AHEAD)
         zero_scales(1)
@@ -234,9 +234,9 @@ def tile_layernormgrucell_pa_k_kernel(
                 nc.tensor.matmul(out=spread[:], lhsT=ones[:], rhs=bias_rows[:, which, cols], start=True, stop=True)
                 nc.scalar.copy(out=bias[:, which, cols], in_=spread[:])
 
-        h_grouped = keep.tile([P, 1, ROW_TILES, P, PACK], BF16, name="h_grouped", align_bytes=64)
-        h_codes = keep.tile([P, 1, B], U32, name="h_codes", align_bytes=64)
-        h_scales = keep.tile([P, 1, B], U8, name="h_scales", align_bytes=64)
+        h_grouped = keep.tile([P, 1, ROW_TILES, P, PACK], BF16, name="h_grouped", align_bytes=256)
+        h_codes = keep.tile([P, 1, B], U32, name="h_codes", align_bytes=256)
+        h_scales = keep.tile([P, 1, B], U8, name="h_scales", align_bytes=256)
         empty_banks(nc, transpose_groups(nc, banks, even_and_odd_words(h_raw), identity), h_grouped)
         for c in range(AHEAD):
             sort_x(c, nc.vector.tensor_copy)

@@ -32,6 +32,8 @@ CHUNK_START = [sum(CHUNK_GROUPS[:c]) for c in range(CHUNKS)]
 AHEAD = 2
 X_BUFS = AHEAD + 1
 SCALAR_BANKS = 2
+COUNT_PIECES = 2
+LAST_PIECE = 256
 LAST_CHUNKS = 2
 
 
@@ -103,13 +105,16 @@ def count(nc, stats, v, half):
     nc.vector.bn_stats(out=stats[:, half, :], in_=v[:, half_columns(half)])
 
 
+def add_eps(nc, stats):
+    third = stats[:, 0, 2:3]
+    nc.vector.tensor_scalar(out=third, in0=third, scalar1=G * EPS, scalar2=None, op0=ALU.add)
+
+
 def rstd_and_shift(nc, pool, stats, minus_half):
     mean_var = pool.tile([P, 2], F32, name="mean_var")
     nc.vector.bn_aggr(out=mean_var[:], in_=stats[:].rearrange("p h s -> p (h s)"))
-    var_eps = pool.tile([P, 1], F32, name="var_eps")
-    nc.vector.tensor_scalar(out=var_eps[:], in0=mean_var[:, 1:2], scalar1=EPS, scalar2=None, op0=ALU.add)
     rstd = pool.tile([P, 1], F32, name="rstd")
-    nc.gpsimd.tensor_tensor(out=rstd[:], in0=var_eps[:], in1=minus_half[:], op=ALU.pow)
+    nc.gpsimd.tensor_tensor(out=rstd[:], in0=mean_var[:, 1:2], in1=minus_half[:], op=ALU.pow)
     shift = pool.tile([P, 1], F32, name="shift")
     nc.gpsimd.tensor_scalar(
         out=shift[:], in0=mean_var[:, 0:1], scalar1=rstd[:, 0:1], scalar2=-1.0, op0=ALU.mult, op1=ALU.mult
@@ -129,8 +134,8 @@ def tile_layernormgrucell_pa_k_kernel(
         grouped_pool = ctx.enter_context(tc.tile_pool(name="grouped", bufs=2))
         codes_pool = ctx.enter_context(tc.tile_pool(name="codes", bufs=AHEAD + 2))
         norm_pool = ctx.enter_context(tc.tile_pool(name="norm", bufs=2))
-        out_pool = ctx.enter_context(tc.tile_pool(name="out", bufs=2))
-        gate_pool = ctx.enter_context(tc.tile_pool(name="gate", bufs=ROW_TILES * HALVES))
+        out_pool = ctx.enter_context(tc.tile_pool(name="out", bufs=4))
+        gate_pool = ctx.enter_context(tc.tile_pool(name="gate", bufs=G // LAST_PIECE))
         sum_banks = ctx.enter_context(tc.psum_pool(name="sums", bufs=1))
         banks = ctx.enter_context(tc.psum_pool(name="banks", bufs=4))
 
@@ -264,6 +269,7 @@ def tile_layernormgrucell_pa_k_kernel(
             stats = norm_pool.tile([P, HALVES, 6], F32, name="stats")
             for half in range(HALVES):
                 count(nc, stats, h_v[r], half)
+            add_eps(nc, stats)
             rstd, shift = rstd_and_shift(nc, norm_pool, stats, minus_half)
             nc.vector.tensor_scalar(
                 out=h_norm[:, r, :], in0=h_v[r][:], scalar1=rstd[:, 0:1], scalar2=shift[:, 0:1], op0=ALU.mult, op1=ALU.add
@@ -287,16 +293,28 @@ def tile_layernormgrucell_pa_k_kernel(
             multiply_x(1, half, last)
 
         x_v = [norm_pool.tile([P, G], F32, name="v") for r in range(ROW_TILES)]
-        x_stats = [norm_pool.tile([P, HALVES, 6], F32, name="stats") for r in range(ROW_TILES)]
+        x_stats = [norm_pool.tile([P, 1 + COUNT_PIECES, 6], F32, name="x_stats") for r in range(ROW_TILES)]
 
-        def take(r, half):
-            add_bias(nc, x_v[r], x_sums[r], bias[:, 0, :], half)
-            count(nc, x_stats[r], x_v[r], half)
+        def take_first(r):
+            add_bias(nc, x_v[r], x_sums[r], bias[:, 0, :], 0)
+            count(nc, x_stats[r], x_v[r], 0)
 
-        def finish(r, rstd, shift):
-            for half in range(HALVES):
-                cols = half_columns(half)
-                both = out_pool.tile([P, N_TILE], F32, name="both")
+        def take_second(r):
+            width = N_TILE // COUNT_PIECES
+            for i in range(COUNT_PIECES):
+                cols = slice(i * width, (i + 1) * width)
+                v_cols = slice(N_TILE + i * width, N_TILE + (i + 1) * width)
+                nc.vector.tensor_tensor(
+                    out=x_v[r][:, v_cols], in0=x_sums[r][1][:, cols], in1=bias[:, 0, v_cols], op=ALU.add
+                )
+            for i in range(COUNT_PIECES):
+                v_cols = slice(N_TILE + i * width, N_TILE + (i + 1) * width)
+                nc.vector.bn_stats(out=x_stats[r][:, 1 + i, :], in_=x_v[r][:, v_cols])
+
+        def finish(r, rstd, shift, width):
+            for first in range(0, G, width):
+                cols = slice(first, first + width)
+                both = out_pool.tile([P, width], F32, name="both")
                 nc.vector.scalar_tensor_tensor(
                     out=both[:],
                     in0=x_v[r][:, cols],
@@ -305,15 +323,17 @@ def tile_layernormgrucell_pa_k_kernel(
                     op0=ALU.mult,
                     op1=ALU.add,
                 )
-                gate = gate_pool.tile([P, N_TILE], F32, name="gate")
+                gate = gate_pool.tile([P, width], F32, name="gate", tag="gate%d" % width)
                 nc.scalar.activation(out=gate[:], in_=both[:], func=ACT.Sigmoid, bias=shift[:, 0:1])
                 nc.sync.dma_start(out=out[r * P : (r + 1) * P, cols], in_=gate[:])
 
-        take(0, 0)
-        take(0, 1)
+        take_first(0)
+        take_second(0)
+        add_eps(nc, x_stats[0])
         rstd_0, shift_0 = rstd_and_shift(nc, norm_pool, x_stats[0], minus_half)
-        take(1, 0)
-        finish(0, rstd_0, shift_0)
-        take(1, 1)
+        take_first(1)
+        finish(0, rstd_0, shift_0, N_TILE)
+        add_eps(nc, x_stats[1])
+        take_second(1)
         rstd_1, shift_1 = rstd_and_shift(nc, norm_pool, x_stats[1], minus_half)
-        finish(1, rstd_1, shift_1)
+        finish(1, rstd_1, shift_1, LAST_PIECE)

@@ -110,16 +110,12 @@ def add_eps(nc, stats):
     nc.vector.tensor_scalar(out=third, in0=third, scalar1=G * EPS, scalar2=None, op0=ALU.add)
 
 
-def rstd_and_shift(nc, pool, stats, minus_half):
+def mean_and_rstd(nc, pool, stats, minus_half):
     mean_var = pool.tile([P, 2], F32, name="mean_var")
     nc.vector.bn_aggr(out=mean_var[:], in_=stats[:].rearrange("p h s -> p (h s)"))
     rstd = pool.tile([P, 1], F32, name="rstd")
     nc.gpsimd.tensor_tensor(out=rstd[:], in0=mean_var[:, 1:2], in1=minus_half[:], op=ALU.pow)
-    shift = pool.tile([P, 1], F32, name="shift")
-    nc.gpsimd.tensor_scalar(
-        out=shift[:], in0=mean_var[:, 0:1], scalar1=rstd[:, 0:1], scalar2=-1.0, op0=ALU.mult, op1=ALU.mult
-    )
-    return rstd, shift
+    return mean_var[:, 0:1], rstd[:]
 
 
 def tile_layernormgrucell_pa_k_kernel(
@@ -270,9 +266,9 @@ def tile_layernormgrucell_pa_k_kernel(
             for half in range(HALVES):
                 count(nc, stats, h_v[r], half)
             add_eps(nc, stats)
-            rstd, shift = rstd_and_shift(nc, norm_pool, stats, minus_half)
+            mean, rstd = mean_and_rstd(nc, norm_pool, stats, minus_half)
             nc.vector.tensor_scalar(
-                out=h_norm[:, r, :], in0=h_v[r][:], scalar1=rstd[:, 0:1], scalar2=shift[:, 0:1], op0=ALU.mult, op1=ALU.add
+                out=h_norm[:, r, :], in0=h_v[r][:], scalar1=mean, scalar2=rstd, op0=ALU.subtract, op1=ALU.mult
             )
 
         last = list(range(CHUNKS - LAST_CHUNKS, CHUNKS))
@@ -311,18 +307,16 @@ def tile_layernormgrucell_pa_k_kernel(
                 v_cols = slice(N_TILE + i * width, N_TILE + (i + 1) * width)
                 nc.vector.bn_stats(out=x_stats[r][:, 1 + i, :], in_=x_v[r][:, v_cols])
 
-        def finish(r, rstd, shift, width):
+        def finish(r, mean, rstd, width):
+            shift = norm_pool.tile([P, 1], F32, name="shift")
             for first in range(0, G, width):
                 cols = slice(first, first + width)
                 both = out_pool.tile([P, width], F32, name="both")
                 nc.vector.scalar_tensor_tensor(
-                    out=both[:],
-                    in0=x_v[r][:, cols],
-                    scalar=rstd[:, 0:1],
-                    in1=h_norm[:, r, cols],
-                    op0=ALU.mult,
-                    op1=ALU.add,
+                    out=both[:], in0=x_v[r][:, cols], scalar=rstd, in1=h_norm[:, r, cols], op0=ALU.mult, op1=ALU.add
                 )
+                if first == 0:
+                    nc.vector.tensor_scalar(out=shift[:], in0=mean, scalar1=rstd, scalar2=-1.0, op0=ALU.mult, op1=ALU.mult)
                 gate = gate_pool.tile([P, width], F32, name="gate", tag="gate%d" % width)
                 nc.scalar.activation(out=gate[:], in_=both[:], func=ACT.Sigmoid, bias=shift[:, 0:1])
                 nc.sync.dma_start(out=out[r * P : (r + 1) * P, cols], in_=gate[:])
@@ -330,10 +324,10 @@ def tile_layernormgrucell_pa_k_kernel(
         take_first(0)
         take_second(0)
         add_eps(nc, x_stats[0])
-        rstd_0, shift_0 = rstd_and_shift(nc, norm_pool, x_stats[0], minus_half)
+        mean_0, rstd_0 = mean_and_rstd(nc, norm_pool, x_stats[0], minus_half)
         take_first(1)
-        finish(0, rstd_0, shift_0, N_TILE)
+        finish(0, mean_0, rstd_0, N_TILE)
         add_eps(nc, x_stats[1])
         take_second(1)
-        rstd_1, shift_1 = rstd_and_shift(nc, norm_pool, x_stats[1], minus_half)
-        finish(1, rstd_1, shift_1, LAST_PIECE)
+        mean_1, rstd_1 = mean_and_rstd(nc, norm_pool, x_stats[1], minus_half)
+        finish(1, mean_1, rstd_1, LAST_PIECE)

@@ -30,6 +30,7 @@ CHUNK_GROUPS = [4, 4, 4, 4, 4, 4, 4, 4]
 CHUNKS = len(CHUNK_GROUPS)
 CHUNK_START = [sum(CHUNK_GROUPS[:c]) for c in range(CHUNKS)]
 AHEAD = 2
+W_PIECES = [2 if c in (0, CHUNKS - 1) else 1 for c in range(CHUNKS)]
 X_BUFS = AHEAD + 1
 SCALAR_BANKS = 2
 COUNT_PIECES = 2
@@ -154,12 +155,17 @@ def tile_layernormgrucell_pa_k_kernel(
         def load_w(c):
             some = slice(CHUNK_START[c], CHUNK_START[c] + CHUNK_GROUPS[c])
             load_scale_rows(nc, irz_scales[c], W_irz_scales[some])
-            w_words = keep.tile([P, CHUNK_GROUPS[c], 2 * G], U8, name="w_words%d" % c, align_bytes=256)
-            nc.sync.dma_start(
-                out=w_words[:].bitcast(I32), in_=W_irz_words[some].bitcast(I32).rearrange("g p n -> p g n")
-            )
-            for g in range(CHUNK_GROUPS[c]):
-                w_groups.append((w_words[:, g, :], irz_scales[c][:, g, :]))
+            pieces = W_PIECES[c]
+            width = CHUNK_GROUPS[c] // pieces
+            for i in range(pieces):
+                w_words = keep.tile([P, width, 2 * G], U8, name="w_words%d_%d" % (c, i), align_bytes=256)
+                first = CHUNK_START[c] + i * width
+                nc.sync.dma_start(
+                    out=w_words[:].bitcast(I32),
+                    in_=W_irz_words[first : first + width].bitcast(I32).rearrange("g p n -> p g n"),
+                )
+                for g in range(width):
+                    w_groups.append((w_words[:, g, :], irz_scales[c][:, i * width + g, :]))
 
         def sort_x(c, copy):
             sorted_words = sorted_pool.tile([P, ROW_TILES, CHUNK_GROUPS[c], 2, P], F32, name="sorted_words")
@@ -192,8 +198,7 @@ def tile_layernormgrucell_pa_k_kernel(
             for r in range(ROW_TILES)
         ]
 
-        def multiply_x(r, half, chunks):
-            some = [g for c in chunks for g in range(CHUNK_START[c], CHUNK_START[c] + CHUNK_GROUPS[c])]
+        def multiply_x(r, half, some):
             multiply_groups(
                 nc, x_sums[r][half], r, half, [x_groups[g] + w_groups[g] for g in some], some[0] == 0, some[-1] == GROUPS - 1
             )
@@ -271,14 +276,19 @@ def tile_layernormgrucell_pa_k_kernel(
                 out=h_norm[:, r, :], in0=h_v[r][:], scalar1=mean, scalar2=rstd, op0=ALU.subtract, op1=ALU.mult
             )
 
-        last = list(range(CHUNKS - LAST_CHUNKS, CHUNKS))
+        held = []
         for c in range(CHUNKS):
-            for r in range(ROW_TILES):
-                if r == 0 or c not in last:
-                    for half in range(HALVES):
-                        multiply_x(r, half, [c])
-                if c == 0 and r == 0:
-                    multiply_h()
+            width = CHUNK_GROUPS[c] // W_PIECES[c]
+            for i in range(W_PIECES[c]):
+                some = list(range(CHUNK_START[c] + i * width, CHUNK_START[c] + (i + 1) * width))
+                for r in range(ROW_TILES):
+                    if r == 1 and c >= CHUNKS - LAST_CHUNKS:
+                        held.extend(some)
+                    else:
+                        for half in range(HALVES):
+                            multiply_x(r, half, some)
+                    if c == 0 and r == 0 and i == 0:
+                        multiply_h()
             if c + AHEAD < CHUNKS:
                 sort_x(c + AHEAD, nc.scalar.copy)
                 turn_x(c + AHEAD)
@@ -286,7 +296,7 @@ def tile_layernormgrucell_pa_k_kernel(
             if c < ROW_TILES:
                 normalise_h(c)
         for half in range(HALVES):
-            multiply_x(1, half, last)
+            multiply_x(1, half, held)
 
         x_v = [norm_pool.tile([P, G], F32, name="v") for r in range(ROW_TILES)]
         x_stats = [norm_pool.tile([P, 1 + COUNT_PIECES, 6], F32, name="x_stats") for r in range(ROW_TILES)]

from contextlib import ExitStack

import concourse.mybir as mybir
from concourse.masks import make_identity

F32 = mybir.dt.float32
BF16 = mybir.dt.bfloat16
I32 = mybir.dt.int32
U32 = mybir.dt.uint32
U8 = mybir.dt.uint8
FP8X4 = mybir.dt.float8_e4m3fn_x4
FP4X4 = mybir.dt.float4_e2m1fn_x4
ALU = mybir.AluOpType
ACT = mybir.ActivationFunctionType

B, I, H, G = 256, 16384, 512, 1024
EPS = 1e-5
FLOPS = 2 * B * (I + H) * G

P = 128
PACK = 4
K_PASS = P * PACK
ROW_TILES = B // P
N_TILE = 512
HALVES = G // N_TILE
SCALE_ROWS = K_PASS // 32
GROUPS = I // K_PASS

CHUNK_GROUPS = [4, 4, 4, 4, 4, 4, 4, 4]
CHUNKS = len(CHUNK_GROUPS)
CHUNK_START = [sum(CHUNK_GROUPS[:c]) for c in range(CHUNKS)]
AHEAD = 2
W_PIECES = [2 if c in (0, CHUNKS - 1) else 1 for c in range(CHUNKS)]
X_BUFS = AHEAD + 1
SCALAR_BANKS = 2
COUNT_PIECES = 2
LAST_PIECE = 256
LAST_CHUNKS = 2


def load_scale_rows(nc, planes, scales):
    for j in range(4):
        nc.sync.dma_start(
            out=planes[j:P:32, :, :].bitcast(I32),
            in_=scales[:, j:SCALE_ROWS:4, :].bitcast(I32).rearrange("g q n -> q g n"),
        )


def even_and_odd_words(raw):
    return raw[:].bitcast(F32).rearrange("b r (g p u) -> b r g u p", p=P, u=2)


def transpose_groups(nc, banks, words, identity):
    filled = []
    for g in range(words.shape[2]):
        bank = banks.tile([P, ROW_TILES, 2, P], F32, name="bank", tag="bank")
        for r in range(ROW_TILES):
            for u in range(2):
                nc.tensor.transpose(bank[:, r, u, :], words[:, r, g, u, :], identity[:])
        filled.append(bank)
    return filled


def empty_banks(nc, filled, grouped):
    for g, bank in enumerate(filled):
        side_by_side = grouped[:, g].bitcast(F32)
        alternately = bank[:].rearrange("p r u b -> p r b u")
        if g % 4 < SCALAR_BANKS:
            nc.scalar.copy(out=side_by_side, in_=alternately)
        else:
            nc.vector.tensor_copy(out=side_by_side, in_=alternately)


def quantise(nc, grouped, codes, scales):
    nc.vector.quantize_mx(
        out=codes[:].rearrange("p g c -> p (g c)").bitcast(FP8X4),
        scales=scales[:].rearrange("p g c -> p (g c)"),
        in_=grouped[:].rearrange("p g r b t -> p (g r b t)"),
    )


def multiply_groups(nc, total, r, half, groups, first, last):
    rows = slice(r * P, (r + 1) * P)
    for i, (codes, scales, w_words, w_scales) in enumerate(groups):
        nc.tensor.matmul_mx(
            out=total[:],
            lhsT=codes[:, rows].bitcast(FP8X4),
            lhsT_scale=scales[:, rows],
            rhs=w_words[:, half * 2 * N_TILE : (half + 1) * 2 * N_TILE].bitcast(FP4X4),
            rhs_scale=w_scales[:, half * N_TILE : (half + 1) * N_TILE],
            start=first and i == 0,
            stop=last and i == len(groups) - 1,
        )


def half_columns(half):
    return slice(half * N_TILE, (half + 1) * N_TILE)


def add_bias(nc, v, sums_of_rows, bias, half):
    cols = half_columns(half)
    nc.vector.tensor_tensor(out=v[:, cols], in0=sums_of_rows[half][:], in1=bias[:, cols], op=ALU.add)


def count(nc, stats, v, half):
    nc.vector.bn_stats(out=stats[:, half, :], in_=v[:, half_columns(half)])


def add_eps(nc, stats):
    third = stats[:, 0, 2:3]
    nc.vector.tensor_scalar(out=third, in0=third, scalar1=G * EPS, scalar2=None, op0=ALU.add)


def mean_and_rstd(nc, pool, stats, minus_half):
    mean_var = pool.tile([P, 2], F32, name="mean_var")
    nc.vector.bn_aggr(out=mean_var[:], in_=stats[:].rearrange("p h s -> p (h s)"))
    rstd = pool.tile([P, 1], F32, name="rstd")
    nc.gpsimd.tensor_tensor(out=rstd[:], in0=mean_var[:, 1:2], in1=minus_half[:], op=ALU.pow)
    return mean_var[:, 0:1], rstd[:]


def tile_layernormgrucell_pa_k_kernel(
    tc, x, h, W_irz_words, W_irz_scales, b_irz, W_hrz_words, W_hrz_scales, b_hrz, out
):
    nc = tc.nc
    with ExitStack() as ctx:
        ctx.enter_context(tc.manual_schedule())
        keep = ctx.enter_context(tc.tile_pool(name="keep", bufs=1))
        x_pool = ctx.enter_context(tc.tile_pool(name="x", bufs=X_BUFS))
        sorted_pool = ctx.enter_context(tc.tile_pool(name="sorted", bufs=2))
        grouped_pool = ctx.enter_context(tc.tile_pool(name="grouped", bufs=2))
        codes_pool = ctx.enter_context(tc.tile_pool(name="codes", bufs=AHEAD + 2))
        norm_pool = ctx.enter_context(tc.tile_pool(name="norm", bufs=2))
        out_pool = ctx.enter_context(tc.tile_pool(name="out", bufs=4))
        gate_pool = ctx.enter_context(tc.tile_pool(name="gate", bufs=G // LAST_PIECE))
        sum_banks = ctx.enter_context(tc.psum_pool(name="sums", bufs=1))
        banks = ctx.enter_context(tc.psum_pool(name="banks", bufs=4))

        x_rows = x.rearrange("(r p) k -> p r k", p=P)
        x_raw = {}
        x_words = {}
        x_groups = []
        w_groups = []
        irz_scales = {}

        def load_x(c):
            x_raw[c] = x_pool.tile([P, ROW_TILES, CHUNK_GROUPS[c] * K_PASS], BF16, name="x_raw")
            first_k = CHUNK_START[c] * K_PASS
            nc.sync.dma_start(out=x_raw[c][:], in_=x_rows[:, :, first_k : first_k + CHUNK_GROUPS[c] * K_PASS])

        def zero_scales(c):
            irz_scales[c] = keep.tile([P, CHUNK_GROUPS[c], G], U8, name="irz_scales%d" % c, align_bytes=256)
            nc.vector.memset(irz_scales[c][:].bitcast(I32), 0)

        def load_w(c):
            some = slice(CHUNK_START[c], CHUNK_START[c] + CHUNK_GROUPS[c])
            load_scale_rows(nc, irz_scales[c], W_irz_scales[some])
            pieces = W_PIECES[c]
            width = CHUNK_GROUPS[c] // pieces
            for i in range(pieces):
                w_words = keep.tile([P, width, 2 * G], U8, name="w_words%d_%d" % (c, i), align_bytes=256)
                first = CHUNK_START[c] + i * width
                nc.sync.dma_start(
                    out=w_words[:].bitcast(I32),
                    in_=W_irz_words[first : first + width].bitcast(I32).rearrange("g p n -> p g n"),
                )
                for g in range(width):
                    w_groups.append((w_words[:, g, :], irz_scales[c][:, i * width + g, :]))

        def sort_x(c, copy):
            sorted_words = sorted_pool.tile([P, ROW_TILES, CHUNK_GROUPS[c], 2, P], F32, name="sorted_words")
            copy(
                out=sorted_words[:].rearrange("b r g u p -> b (r g) u p"),
                in_=even_and_odd_words(x_raw[c]).rearrange("b r g u p -> b (r g) u p"),
            )
            x_words[c] = sorted_words[:]

        def turn_x(c):
            filled = transpose_groups(nc, banks, x_words[c], identity)
            grouped = grouped_pool.tile([P, CHUNK_GROUPS[c], ROW_TILES, P, PACK], BF16, name="grouped", align_bytes=256)
            x_codes = codes_pool.tile([P, CHUNK_GROUPS[c], B], U32, name="x_codes", align_bytes=256)
            x_scales = codes_pool.tile([P, CHUNK_GROUPS[c], B], U8, name="x_scales", align_bytes=256)
            empty_banks(nc, filled, grouped)
            quantise(nc, grouped, x_codes, x_scales)
            for g in range(CHUNK_GROUPS[c]):
                x_groups.append((x_codes[:, g, :], x_scales[:, g, :]))

        def load_behind(c):
            if c + AHEAD < CHUNKS:
                zero_scales(c + AHEAD)
            if c + X_BUFS < CHUNKS:
                load_x(c + X_BUFS)
            if c + AHEAD < CHUNKS:
                load_w(c + AHEAD)

        x_sums = [
            [sum_banks.tile([P, N_TILE], F32, name="x%d%d" % (r, half), tag="x%d%d" % (r, half)) for half in range(HALVES)]
            for r in range(ROW_TILES)
        ]

        def multiply_x(r, half, some):
            multiply_groups(
                nc, x_sums[r][half], r, half, [x_groups[g] + w_groups[g] for g in some], some[0] == 0, some[-1] == GROUPS - 1
            )

        load_x(0)
        bias_rows = keep.tile([P, 2, G], BF16, name="bias_rows")
        nc.vector.memset(bias_rows[:].rearrange("p w n -> p (w n)").bitcast(F32), 0.0)
        nc.sync.dma_start(out=bias_rows[0:1, 0, :], in_=b_irz.rearrange("(o n) -> o n", o=1))
        nc.sync.dma_start(out=bias_rows[0:1, 1, :], in_=b_hrz.rearrange("(o n) -> o n", o=1))
        h_raw = keep.tile([P, ROW_TILES, H], BF16, name="h_raw")
        nc.sync.dma_start(out=h_raw[:], in_=h.rearrange("(r p) k -> p r k", p=P))
        load_x(1)
        zero_scales(0)
        load_w(0)
        ones = keep.tile([P, P], BF16, name="ones")
        nc.vector.memset(ones[:], 1.0)
        minus_half = keep.tile([P, 1], F32, name="minus_half")
        nc.vector.memset(minus_half[:], -0.5)
        zero = keep.tile([P, 1], F32, name="zero")
        nc.vector.memset(zero[:], 0.0)
        identity = keep.tile([P, P], F32, name="identity")
        make_identity(nc, identity[:])
        warm = keep.tile([P, 1], F32, name="warm")
        nc.scalar.activation(out=warm[:], in_=zero[:], func=ACT.Sigmoid)
        hrz_scales = keep.tile([P, 1, G], U8, name="hrz_scales", align_bytes=256)
        nc.vector.memset(hrz_scales[:].bitcast(I32), 0)
        load_scale_rows(nc, hrz_scales, W_hrz_scales)
        hrz_words = keep.tile([P, 1, 2 * G], U8, name="hrz_words", align_bytes=256)
        nc.sync.dma_start(out=hrz_words[:].bitcast(I32), in_=W_hrz_words.bitcast(I32).rearrange("g p n -> p g n"))
        load_x(AHEAD)
        zero_scales(1)
        load_w(1)

        bias = keep.tile([P, 2, G], F32, name="bias")
        for which in range(2):
            for half in range(HALVES):
                cols = half_columns(half)
                spread = banks.tile([P, N_TILE], F32, name="spread", tag="bank")
                nc.tensor.matmul(out=spread[:], lhsT=ones[:], rhs=bias_rows[:, which, cols], start=True, stop=True)
                nc.scalar.copy(out=bias[:, which, cols], in_=spread[:])

        h_grouped = keep.tile([P, 1, ROW_TILES, P, PACK], BF16, name="h_grouped", align_bytes=256)
        h_codes = keep.tile([P, 1, B], U32, name="h_codes", align_bytes=256)
        h_scales = keep.tile([P, 1, B], U8, name="h_scales", align_bytes=256)
        empty_banks(nc, transpose_groups(nc, banks, even_and_odd_words(h_raw), identity), h_grouped)
        for c in range(AHEAD):
            sort_x(c, nc.vector.tensor_copy)
        for c in range(AHEAD):
            turn_x(c)
            if c == 0:
                quantise(nc, h_grouped, h_codes, h_scales)
            load_behind(c)

        h_v = []

        def multiply_h():
            h_groups = [(h_codes[:, 0, :], h_scales[:, 0, :], hrz_words[:, 0, :], hrz_scales[:, 0, :])]
            for r in range(ROW_TILES):
                h_v.append(norm_pool.tile([P, G], F32, name="v"))
                h_sums = []
                for half in range(HALVES):
                    h_sums.append(banks.tile([P, N_TILE], F32, name="h_sum", tag="bank"))
                    multiply_groups(nc, h_sums[half], r, half, h_groups, True, True)
                    add_bias(nc, h_v[r], h_sums, bias[:, 1, :], half)

        h_norm = keep.tile([P, ROW_TILES, G], F32, name="h_norm")

        def normalise_h(r):
            stats = norm_pool.tile([P, HALVES, 6], F32, name="stats")
            for half in range(HALVES):
                count(nc, stats, h_v[r], half)
            add_eps(nc, stats)
            mean, rstd = mean_and_rstd(nc, norm_pool, stats, minus_half)
            nc.vector.tensor_scalar(
                out=h_norm[:, r, :], in0=h_v[r][:], scalar1=mean, scalar2=rstd, op0=ALU.subtract, op1=ALU.mult
            )

        held = []
        for c in range(CHUNKS):
            width = CHUNK_GROUPS[c] // W_PIECES[c]
            for i in range(W_PIECES[c]):
                some = list(range(CHUNK_START[c] + i * width, CHUNK_START[c] + (i + 1) * width))
                for r in range(ROW_TILES):
                    if r == 1 and c >= CHUNKS - LAST_CHUNKS:
                        held.extend(some)
                    else:
                        for half in range(HALVES):
                            multiply_x(r, half, some)
                    if c == 0 and r == 0 and i == 0:
                        multiply_h()
            if c + AHEAD < CHUNKS:
                sort_x(c + AHEAD, nc.scalar.copy)
                turn_x(c + AHEAD)
                load_behind(c + AHEAD)
            if c < ROW_TILES:
                normalise_h(c)
        for half in range(HALVES):
            multiply_x(1, half, held)

        x_v = [norm_pool.tile([P, G], F32, name="v") for r in range(ROW_TILES)]
        x_stats = [norm_pool.tile([P, 1 + COUNT_PIECES, 6], F32, name="x_stats") for r in range(ROW_TILES)]

        def take_first(r):
            add_bias(nc, x_v[r], x_sums[r], bias[:, 0, :], 0)
            count(nc, x_stats[r], x_v[r], 0)

        def take_second(r):
            width = N_TILE // COUNT_PIECES
            for i in range(COUNT_PIECES):
                cols = slice(i * width, (i + 1) * width)
                v_cols = slice(N_TILE + i * width, N_TILE + (i + 1) * width)
                nc.vector.tensor_tensor(
                    out=x_v[r][:, v_cols], in0=x_sums[r][1][:, cols], in1=bias[:, 0, v_cols], op=ALU.add
                )
            for i in range(COUNT_PIECES):
                v_cols = slice(N_TILE + i * width, N_TILE + (i + 1) * width)
                nc.vector.bn_stats(out=x_stats[r][:, 1 + i, :], in_=x_v[r][:, v_cols])

        def finish(r, mean, rstd, width):
            shift = norm_pool.tile([P, 1], F32, name="shift")
            for first in range(0, G, width):
                cols = slice(first, first + width)
                both = out_pool.tile([P, width], F32, name="both")
                nc.vector.scalar_tensor_tensor(
                    out=both[:], in0=x_v[r][:, cols], scalar=rstd, in1=h_norm[:, r, cols], op0=ALU.mult, op1=ALU.add
                )
                if first == 0:
                    nc.vector.tensor_scalar(out=shift[:], in0=mean, scalar1=rstd, scalar2=-1.0, op0=ALU.mult, op1=ALU.mult)
                gate = gate_pool.tile([P, width], F32, name="gate", tag="gate%d" % width)
                nc.scalar.activation(out=gate[:], in_=both[:], func=ACT.Sigmoid, bias=shift[:, 0:1])
                nc.sync.dma_start(out=out[r * P : (r + 1) * P, cols], in_=gate[:])

        take_first(0)
        take_second(0)
        add_eps(nc, x_stats[0])
        mean_0, rstd_0 = mean_and_rstd(nc, norm_pool, x_stats[0], minus_half)
        take_first(1)
        finish(0, mean_0, rstd_0, N_TILE)
        add_eps(nc, x_stats[1])
        take_second(1)
        mean_1, rstd_1 = mean_and_rstd(nc, norm_pool, x_stats[1], minus_half)
        finish(1, mean_1, rstd_1, LAST_PIECE)
